import numpy as np
import ml_dtypes


def mxq(x, axis, fmt="e4m3"):
    dtype, down = {"e4m3": (ml_dtypes.float8_e4m3fn, 7), "e5m2": (ml_dtypes.float8_e5m2, 14)}[fmt]
    v = np.moveaxis(np.asarray(x, np.float32).astype(ml_dtypes.bfloat16).astype(np.float64), axis, -1)
    blocks = v.reshape(v.shape[:-1] + (-1, 32))
    amax = np.abs(blocks).max(-1, keepdims=True)
    byte = np.maximum(np.where(amax > 0, np.frexp(amax)[1] - 1 + 127, 0) - down, 1)
    scale = np.exp2(byte - 127.0)
    codes = (blocks / scale).astype(np.float32).astype(dtype).astype(np.float64)
    return np.moveaxis((codes * scale).reshape(v.shape), -1, axis)


WIDE = False


def mx_kscale(k):
    if not WIDE:
        return np.ones(k)
    levels = np.array([10, -10, 5, -5, 0])
    a = np.random.permutation(np.resize(levels, k // 512 * 4)).reshape(k // 512, 4)
    idx = np.arange(k)
    return np.exp2(a[idx // 512, idx % 128 // 32])


BF16 = ml_dtypes.bfloat16


def bf(x):
    return np.asarray(x, np.float32).astype(BF16)


def f64(x):
    return np.asarray(x).astype(np.float64)


B, S, D, E, F, NH, BAND = 4, 256, 512, 512, 1024, 4, 6
HL = D // NH
HG = E // NH
EPS = 1e-5


def layernorm(x, w, b):
    m = x.mean(-1, keepdims=True)
    v = ((x - m) ** 2).mean(-1, keepdims=True)
    return (x - m) / np.sqrt(v + EPS) * w + b


def heads(t):
    return t.reshape(B, S, NH, HG).transpose(0, 2, 1, 3)


def setup_inputs():
    r = np.random.standard_normal
    s = mx_kscale(D)
    return {
        "o_loc": bf(r((B, NH, S, HL)) * 0.5 * s.reshape(NH, 1, HL)),
        "x": bf(r((B, S, D))),
        "Wo_l": bf(r((D, D)) / np.sqrt(D) / s),
        "bo_l": bf(r(D) * 0.1),
        "ln2_w": bf(1.0 + 0.1 * r(D)),
        "ln2_b": bf(r(D) * 0.1),
        "Wqkv_g": bf(r((3 * E, D)) * 1.4 / np.sqrt(D)),
        "bqkv_g": bf(r(3 * E) * 0.1),
    }


def reference(o_loc, x, Wo_l, bo_l, ln2_w, ln2_b, Wqkv_g, bqkv_g):
    o = f64(o_loc).transpose(0, 2, 1, 3).reshape(B, S, D)
    x_loc = f64(x) + ((mxq(o, 2, "e4m3") @ mxq(f64(Wo_l), 1, "e4m3").T) + f64(bo_l))
    h = layernorm(x_loc, f64(ln2_w), f64(ln2_b))
    qkv = (mxq(h, 2, "e4m3") @ mxq(f64(Wqkv_g), 1, "e4m3").T) + f64(bqkv_g)
    q, k, v = np.split(qkv, 3, axis=-1)
    return x_loc, heads(q), heads(k), heads(v)

@@ -1,0 +1,276 @@
+from contextlib import ExitStack
+
+import concourse.mybir as mybir
+from concourse.masks import make_identity
+
+F32 = mybir.dt.float32
+BF16 = mybir.dt.bfloat16
+U32 = mybir.dt.uint32
+U8 = mybir.dt.uint8
+FP8X4 = mybir.dt.float8_e4m3fn_x4
+ACT = mybir.ActivationFunctionType
+ALU = mybir.AluOpType
+
+P = 128
+B = 4
+S = 256
+D = 512
+NH = 4
+HD = 128
+J = S // P
+WORDS = D // 2
+N_QKV = 3
+EPS = 1e-5
+
+FLOPS = 2 * B * S * D * (D + N_QKV * D)
+
+
+def tile_block_pa_kernel(
+    tc, o_loc, x, Wo_l, bo_l, ln2_w, ln2_b, Wqkv_g, bqkv_g, out_0, out_1, out_2, out_3
+):
+    nc = tc.nc
+    qkv_out = [out_1, out_2, out_3]
+
+    with ExitStack() as stack:
+        keep = stack.enter_context(tc.tile_pool(name="keep", bufs=1))
+        stage = stack.enter_context(tc.tile_pool(name="stage", bufs=2))
+        results = stack.enter_context(tc.tile_pool(name="results", bufs=4))
+        psum = stack.enter_context(tc.psum_pool(name="psum", bufs=2))
+
+        ident = keep.tile([P, P], F32)
+        make_identity(nc, ident[:])
+        ln_rows = keep.tile([P, 2 * P], BF16)
+        nc.vector.memset(ln_rows[:], 0.0)
+
+        o_sb = [keep.tile([P, J * D], BF16, name="o_sb%d" % b) for b in range(B)]
+        x_sb = [keep.tile([P, J * D], BF16, name="x_sb%d" % b) for b in range(B)]
+        wo_sb = keep.tile([P, 4 * D], BF16)
+        wqkv_sb = [keep.tile([P, 4 * D], BF16, name="wqkv_sb%d" % c) for c in range(N_QKV)]
+        bo_bc = keep.tile([P, D], BF16)
+        bq_bc = keep.tile([P, N_QKV * D], BF16)
+
+        def load_o(b):
+            for j in range(J):
+                nc.sync.dma_start(
+                    out=o_sb[b][:, j * D : (j + 1) * D].rearrange("p (n d) -> p n d", n=NH),
+                    in_=o_loc[b].rearrange("n (p j) d -> p j n d", j=J)[:, j],
+                )
+
+        def load_x(b):
+            nc.sync.dma_start(out=x_sb[b][:], in_=x[b].rearrange("(p j) d -> p (j d)", j=J))
+
+        def load_weight(w_sb, rows):
+            nc.sync.dma_start(
+                out=w_sb[:].rearrange("p (t k) -> p t k", k=D),
+                in_=rows.rearrange("(t p) k -> p t k", p=P),
+            )
+
+        load_o(0)
+        load_weight(wo_sb, Wo_l)
+        load_x(0)
+        nc.scalar.dma_start(out=bo_bc[:], in_=bo_l.partition_broadcast(P))
+        nc.scalar.dma_start(out=ln_rows[0:2, :], in_=ln2_w.rearrange("(u c) -> u c", u=2))
+        nc.scalar.dma_start(out=ln_rows[2:4, :], in_=ln2_b.rearrange("(u c) -> u c", u=2))
+        for c in range(N_QKV):
+            load_weight(wqkv_sb[c], Wqkv_g[c * D : (c + 1) * D, :])
+        nc.scalar.dma_start(out=bq_bc[:], in_=bqkv_g.partition_broadcast(P))
+        for b in range(1, B):
+            load_o(b)
+            load_x(b)
+
+        def copy_words(which, out, in_):
+            if which % 2 == 0:
+                nc.scalar.copy(out=out, in_=in_)
+            else:
+                nc.vector.tensor_copy(out=out, in_=in_)
+
+        def quantise_weight(w_sb, codes, scales):
+            words = w_sb[:].bitcast(F32)
+            grouped = stage.tile([P, 4 * D], BF16, align_bytes=64, name="grouped_w")
+            grouped_words = grouped[:].bitcast(F32).rearrange("q (t p u) -> q t p u", t=4, u=2)
+            for half in range(2):
+                bank = psum.tile([P, 2, 2, P], F32, name="tr_bank", tag="tr")
+                for tt in range(2):
+                    for u in range(2):
+                        start = (2 * half + tt) * WORDS + u * P
+                        nc.tensor.transpose(bank[:, tt, u, :], words[:, start : start + P], ident[:])
+                copy_words(
+                    half,
+                    grouped_words[:, 2 * half : 2 * half + 2],
+                    bank[:].rearrange("q t u p -> q t p u"),
+                )
+            nc.vector.quantize_mx(out=codes.bitcast(FP8X4), scales=scales, in_=grouped[:])
+
+        o_codes = [None] * B
+        o_scales = [None] * B
+        xb = [None] * B
+
+        def prepare_o(b):
+            words = o_sb[b][:].bitcast(F32)
+            bank = psum.tile([P, J, 2, P], F32, name="tr_bank", tag="tr")
+            for j in range(J):
+                for u in range(2):
+                    start = j * WORDS + u * P
+                    nc.tensor.transpose(bank[:, j, u, :], words[:, start : start + P], ident[:])
+            grouped = stage.tile([P, J * D], BF16, align_bytes=64, name="grouped_o")
+            nc.scalar.copy(
+                out=grouped[:].bitcast(F32).rearrange("q (j s u) -> q j s u", j=J, u=2),
+                in_=bank[:].rearrange("q j u s -> q j s u"),
+            )
+            o_codes[b] = stage.tile([P, J * P], U32, align_bytes=64, name="o_codes")
+            o_scales[b] = stage.tile([P, J * P], U8, align_bytes=64, name="o_scales")
+            nc.vector.quantize_mx(
+                out=o_codes[b][:].bitcast(FP8X4), scales=o_scales[b][:], in_=grouped[:]
+            )
+            xb[b] = stage.tile([P, J, D], F32, name="xb")
+            nc.gpsimd.tensor_tensor(
+                out=xb[b][:],
+                in0=x_sb[b][:].rearrange("p (j d) -> p j d", j=J),
+                in1=bo_bc[:].unsqueeze(1).to_broadcast([P, J, D]),
+                op=ALU.add,
+            )
+
+        x_loc = [None] * B
+        sums = [None] * B
+
+        def first_product(b):
+            x_loc[b] = results.tile([P, J, D], F32, name="x_loc")
+            sums[b] = stage.tile([P, J], F32, name="sums")
+            for j in range(J):
+                acc = psum.tile([P, D], F32, name="acc1", tag="acc1")
+                nc.tensor.matmul_mx(
+                    out=acc[:],
+                    lhsT=o_codes[b][:, j * P : (j + 1) * P].bitcast(FP8X4),
+                    lhsT_scale=o_scales[b][:, j * P : (j + 1) * P],
+                    rhs=wo_codes[:].bitcast(FP8X4),
+                    rhs_scale=wo_scales[:],
+                    start=True,
+                    stop=True,
+                )
+                nc.vector.scalar_tensor_tensor(
+                    out=x_loc[b][:, j, :],
+                    in0=acc[:],
+                    scalar=1.0,
+                    in1=xb[b][:, j, :],
+                    op0=ALU.mult,
+                    op1=ALU.add,
+                    accum_out=sums[b][:, j : j + 1],
+                )
+            nc.sync.dma_start(
+                out=out_0[b].rearrange("(p j) d -> p (j d)", j=J),
+                in_=x_loc[b][:].rearrange("p j d -> p (j d)"),
+            )
+
+        def normalise_and_quantise(b):
+            neg_mean = stage.tile([P, J], F32, name="neg_mean")
+            nc.scalar.mul(out=neg_mean[:], in_=sums[b][:], mul=-1.0 / D)
+            sum_sq = stage.tile([P, J], F32, name="sum_sq")
+            for j in range(J):
+                squares = stage.tile([P, D], BF16, name="squares")
+                nc.scalar.activation(
+                    out=squares[:],
+                    in_=x_loc[b][:, j, :],
+                    func=ACT.Square,
+                    bias=neg_mean[:, j : j + 1],
+                    scale=1.0,
+                    accum_out=sum_sq[:, j : j + 1],
+                )
+            std = stage.tile([P, J], F32, name="std")
+            nc.scalar.activation(out=std[:], in_=sum_sq[:], func=ACT.Sqrt, bias=eps_col[:], scale=1.0 / D)
+            rstd = stage.tile([P, J], F32, name="rstd")
+            nc.vector.reciprocal(out=rstd[:], in_=std[:])
+            shift = stage.tile([P, J], F32, name="shift")
+            nc.vector.tensor_mul(out=shift[:], in0=neg_mean[:], in1=rstd[:])
+            normed = stage.tile([P, J, 2, WORDS], F32, name="normed")
+            for j in range(J):
+                nc.scalar.activation(
+                    out=normed[:, j],
+                    in_=x_loc[b][:, j, :].rearrange("p (c e) -> p e c", e=2),
+                    func=ACT.Identity,
+                    bias=shift[:, j : j + 1],
+                    scale=rstd[:, j : j + 1],
+                )
+            h_t = stage.tile([P, 4, S], BF16, name="h_t")
+            for u in range(2):
+                bank = psum.tile([P, 2, S], F32, name="ht_bank", tag="ht")
+                for e in range(2):
+                    for j in range(J):
+                        nc.tensor.transpose(
+                            bank[:, e, j * P : (j + 1) * P],
+                            normed[:, j, e, u * P : (u + 1) * P],
+                            ident[:],
+                        )
+                for e in range(2):
+                    t = 2 * u + e
+                    nc.scalar.activation(
+                        out=h_t[:, t, :],
+                        in_=bank[:, e, :],
+                        func=ACT.Identity,
+                        bias=ln_cols[:, 4 + t : 5 + t],
+                        scale=ln_cols[:, t : t + 1],
+                    )
+            grouped = stage.tile([P, S, 4], BF16, align_bytes=64, name="grouped_h")
+            nc.vector.tensor_copy(out=grouped[:], in_=h_t[:].rearrange("q t s -> q s t"))
+            h_codes = stage.tile([P, S], U32, align_bytes=64, name="h_codes")
+            h_scales = stage.tile([P, S], U8, align_bytes=64, name="h_scales")
+            nc.vector.quantize_mx(
+                out=h_codes[:].bitcast(FP8X4),
+                scales=h_scales[:],
+                in_=grouped[:].rearrange("q s t -> q (s t)"),
+            )
+            return h_codes, h_scales
+
+        def second_product(b, h_codes, h_scales):
+            for c in range(N_QKV):
+                cols = slice(c * D, (c + 1) * D)
+                heads = results.tile([P, NH, J, HD], F32, name="heads")
+                for j in range(J):
+                    acc = psum.tile([P, D], F32, name="acc2", tag="acc2")
+                    nc.tensor.matmul_mx(
+                        out=acc[:],
+                        lhsT=h_codes[:, j * P : (j + 1) * P].bitcast(FP8X4),
+                        lhsT_scale=h_scales[:, j * P : (j + 1) * P],
+                        rhs=wqkv_codes[:, cols].bitcast(FP8X4),
+                        rhs_scale=wqkv_scales[:, cols],
+                        start=True,
+                        stop=True,
+                    )
+                    nc.vector.tensor_tensor(
+                        out=heads[:, :, j, :],
+                        in0=acc[:].rearrange("p (n d) -> p n d", n=NH),
+                        in1=bq_bc[:, cols].rearrange("p (n d) -> p n d", n=NH),
+                        op=ALU.add,
+                    )
+                nc.sync.dma_start(
+                    out=qkv_out[c][b].rearrange("n (p j) d -> p n (j d)", j=J),
+                    in_=heads[:].rearrange("p n j d -> p n (j d)"),
+                )
+
+        eps_col = keep.tile([P, 1], F32)
+        nc.vector.memset(eps_col[:], EPS)
+        wo_codes = keep.tile([P, D], U32, align_bytes=64)
+        wo_scales = keep.tile([P, D], U8, align_bytes=64)
+        wqkv_codes = keep.tile([P, N_QKV * D], U32, align_bytes=64)
+        wqkv_scales = keep.tile([P, N_QKV * D], U8, align_bytes=64)
+
+        prepare_o(0)
+        quantise_weight(wo_sb, wo_codes[:], wo_scales[:])
+        first_product(0)
+
+        ln_bank = psum.tile([P, P], F32, name="tr_bank", tag="tr")
+        nc.tensor.transpose(ln_bank[:], ln_rows[:].bitcast(F32), ident[:])
+        ln_pairs = keep.tile([P, 8], BF16)
+        nc.vector.tensor_copy(out=ln_pairs[:].bitcast(F32), in_=ln_bank[:, 0:4])
+        ln_cols = keep.tile([P, 8], F32)
+        nc.vector.tensor_copy(out=ln_cols[:], in_=ln_pairs[:])
+
+        for c in range(N_QKV):
+            cols = slice(c * D, (c + 1) * D)
+            quantise_weight(wqkv_sb[c], wqkv_codes[:, cols], wqkv_scales[:, cols])
+
+        for b in range(B):
+            if b + 1 < B:
+                prepare_o(b + 1)
+                first_product(b + 1)
+            h_codes, h_scales = normalise_and_quantise(b)
+            second_product(b, h_codes, h_scales)

@@ -41,13 +41,18 @@ def tile_block_pa_kernel(
         make_identity(nc, ident[:])
         ln_rows = keep.tile([P, 2 * P], BF16)
         nc.vector.memset(ln_rows[:], 0.0)
+        bias_rows = keep.tile([P, 4 * D], BF16)
+        nc.vector.memset(bias_rows[:], 0.0)
+        ones = keep.tile([P, P], BF16)
+        nc.vector.memset(ones[:], 1.0)
 
         o_sb = [keep.tile([P, J * D], BF16, name="o_sb%d" % b) for b in range(B)]
         x_sb = [keep.tile([P, J * D], BF16, name="x_sb%d" % b) for b in range(B)]
         wo_sb = keep.tile([P, 4 * D], BF16)
         wqkv_sb = [keep.tile([P, 4 * D], BF16, name="wqkv_sb%d" % c) for c in range(N_QKV)]
-        bo_bc = keep.tile([P, D], BF16)
-        bq_bc = keep.tile([P, N_QKV * D], BF16)
+        bias_bc = keep.tile([P, 4 * D], BF16)
+        bo_bc = bias_bc[:, 0:D]
+        bq_bc = bias_bc[:, D : 4 * D]
 
         def load_o(b):
             for j in range(J):
@@ -68,12 +73,14 @@ def tile_block_pa_kernel(
         load_o(0)
         load_weight(wo_sb, Wo_l)
         load_x(0)
-        nc.scalar.dma_start(out=bo_bc[:], in_=bo_l.partition_broadcast(P))
+        nc.scalar.dma_start(out=bias_rows[0:1, 0:D], in_=bo_l.rearrange("(o d) -> o d", o=1))
         nc.scalar.dma_start(out=ln_rows[0:2, :], in_=ln2_w.rearrange("(u c) -> u c", u=2))
         nc.scalar.dma_start(out=ln_rows[2:4, :], in_=ln2_b.rearrange("(u c) -> u c", u=2))
         for c in range(N_QKV):
             load_weight(wqkv_sb[c], Wqkv_g[c * D : (c + 1) * D, :])
-        nc.scalar.dma_start(out=bq_bc[:], in_=bqkv_g.partition_broadcast(P))
+        nc.scalar.dma_start(
+            out=bias_rows[0:1, D : 4 * D], in_=bqkv_g.rearrange("(o d) -> o d", o=1)
+        )
         for b in range(1, B):
             load_o(b)
             load_x(b)
@@ -101,6 +108,12 @@ def tile_block_pa_kernel(
                 )
             nc.vector.quantize_mx(out=codes.bitcast(FP8X4), scales=scales, in_=grouped[:])
 
+        def spread_bias(i):
+            cols = slice(i * D, (i + 1) * D)
+            bank = psum.tile([P, D], F32, name="tr_bank", tag="tr")
+            nc.tensor.matmul(out=bank[:], lhsT=ones[:], rhs=bias_rows[:, cols], start=True, stop=True)
+            nc.vector.tensor_copy(out=bias_bc[:, cols], in_=bank[:])
+
         o_codes = [None] * B
         o_scales = [None] * B
         xb = [None] * B
@@ -126,7 +139,7 @@ def tile_block_pa_kernel(
             nc.gpsimd.tensor_tensor(
                 out=xb[b][:],
                 in0=x_sb[b][:].rearrange("p (j d) -> p j d", j=J),
-                in1=bo_bc[:].unsqueeze(1).to_broadcast([P, J, D]),
+                in1=bo_bc.unsqueeze(1).to_broadcast([P, J, D]),
                 op=ALU.add,
             )
 
@@ -253,6 +266,7 @@ def tile_block_pa_kernel(
         wqkv_codes = keep.tile([P, N_QKV * D], U32, align_bytes=64)
         wqkv_scales = keep.tile([P, N_QKV * D], U8, align_bytes=64)
 
+        spread_bias(0)
         prepare_o(0)
         quantise_weight(wo_sb, wo_codes[:], wo_scales[:])
         first_product(0)
@@ -265,6 +279,7 @@ def tile_block_pa_kernel(
         nc.vector.tensor_copy(out=ln_cols[:], in_=ln_pairs[:])
 
         for c in range(N_QKV):
+            spread_bias(1 + c)
             cols = slice(c * D, (c + 1) * D)
             quantise_weight(wqkv_sb[c], wqkv_codes[:, cols], wqkv_scales[:, cols])
 

@@ -10,6 +10,7 @@ U8 = mybir.dt.uint8
 FP8X4 = mybir.dt.float8_e4m3fn_x4
 ACT = mybir.ActivationFunctionType
 ALU = mybir.AluOpType
+RSQRT = ACT.Abs_reciprocal_sqrt
 
 P = 128
 B = 4
@@ -35,33 +36,33 @@ def tile_block_pa_kernel(
         keep = stack.enter_context(tc.tile_pool(name="keep", bufs=1))
         stage = stack.enter_context(tc.tile_pool(name="stage", bufs=2))
         results = stack.enter_context(tc.tile_pool(name="results", bufs=4))
-        psum = stack.enter_context(tc.psum_pool(name="psum", bufs=2))
+        turn_banks = stack.enter_context(tc.psum_pool(name="turn_banks", bufs=3))
+        sum_banks = stack.enter_context(tc.psum_pool(name="sum_banks", bufs=5))
 
-        ident = keep.tile([P, P], F32)
-        make_identity(nc, ident[:])
+        bo_rows = keep.tile([P, D], BF16)
+        nc.vector.memset(bo_rows[:], 0.0)
         ln_rows = keep.tile([P, 2 * P], BF16)
         nc.vector.memset(ln_rows[:], 0.0)
-        bias_rows = keep.tile([P, 4 * D], BF16)
-        nc.vector.memset(bias_rows[:], 0.0)
+        eps_col = keep.tile([P, 1], F32)
+        nc.vector.memset(eps_col[:], EPS)
         ones = keep.tile([P, P], BF16)
         nc.vector.memset(ones[:], 1.0)
+        bq_rows = keep.tile([P, N_QKV * D], BF16)
+        nc.vector.memset(bq_rows[:], 0.0)
+        ident = keep.tile([P, P], F32)
+        make_identity(nc, ident[:])
 
         o_sb = [keep.tile([P, J * D], BF16, name="o_sb%d" % b) for b in range(B)]
         x_sb = [keep.tile([P, J * D], BF16, name="x_sb%d" % b) for b in range(B)]
         wo_sb = keep.tile([P, 4 * D], BF16)
         wqkv_sb = [keep.tile([P, 4 * D], BF16, name="wqkv_sb%d" % c) for c in range(N_QKV)]
-        bias_bc = keep.tile([P, 4 * D], BF16)
-        bo_bc = bias_bc[:, 0:D]
-        bq_bc = bias_bc[:, D : 4 * D]
 
-        def load_o(b):
+        def load_o_and_x(b):
             for j in range(J):
                 nc.sync.dma_start(
                     out=o_sb[b][:, j * D : (j + 1) * D].rearrange("p (n d) -> p n d", n=NH),
                     in_=o_loc[b].rearrange("n (p j) d -> p j n d", j=J)[:, j],
                 )
-
-        def load_x(b):
             nc.sync.dma_start(out=x_sb[b][:], in_=x[b].rearrange("(p j) d -> p (j d)", j=J))
 
         def load_weight(w_sb, rows):
@@ -70,61 +71,62 @@ def tile_block_pa_kernel(
                 in_=rows.rearrange("(t p) k -> p t k", p=P),
             )
 
-        load_o(0)
-        load_weight(wo_sb, Wo_l)
-        load_x(0)
-        nc.scalar.dma_start(out=bias_rows[0:1, 0:D], in_=bo_l.rearrange("(o d) -> o d", o=1))
+        nc.scalar.dma_start(out=bo_rows[0:1, :], in_=bo_l.rearrange("(o d) -> o d", o=1))
         nc.scalar.dma_start(out=ln_rows[0:2, :], in_=ln2_w.rearrange("(u c) -> u c", u=2))
         nc.scalar.dma_start(out=ln_rows[2:4, :], in_=ln2_b.rearrange("(u c) -> u c", u=2))
+        nc.scalar.dma_start(out=bq_rows[0:1, :], in_=bqkv_g.rearrange("(o d) -> o d", o=1))
+        load_weight(wo_sb, Wo_l)
+        load_o_and_x(0)
+        load_o_and_x(1)
         for c in range(N_QKV):
             load_weight(wqkv_sb[c], Wqkv_g[c * D : (c + 1) * D, :])
-        nc.scalar.dma_start(
-            out=bias_rows[0:1, D : 4 * D], in_=bqkv_g.rearrange("(o d) -> o d", o=1)
-        )
-        for b in range(1, B):
-            load_o(b)
-            load_x(b)
+        load_o_and_x(2)
+        load_o_and_x(3)
 
-        def copy_words(which, out, in_):
-            if which % 2 == 0:
-                nc.scalar.copy(out=out, in_=in_)
-            else:
-                nc.vector.tensor_copy(out=out, in_=in_)
+        warm = keep.tile([P, 1], F32)
+        nc.scalar.activation(out=warm[:], in_=eps_col[:], func=RSQRT)
+
+        def turn_words(bank, words, first_word):
+            nc.tensor.transpose(bank, words[:, first_word : first_word + P], ident[:])
 
         def quantise_weight(w_sb, codes, scales):
             words = w_sb[:].bitcast(F32)
             grouped = stage.tile([P, 4 * D], BF16, align_bytes=64, name="grouped_w")
             grouped_words = grouped[:].bitcast(F32).rearrange("q (t p u) -> q t p u", t=4, u=2)
             for half in range(2):
-                bank = psum.tile([P, 2, 2, P], F32, name="tr_bank", tag="tr")
+                bank = turn_banks.tile([P, 2, 2, P], F32, name="w_bank", tag="turn")
                 for tt in range(2):
                     for u in range(2):
-                        start = (2 * half + tt) * WORDS + u * P
-                        nc.tensor.transpose(bank[:, tt, u, :], words[:, start : start + P], ident[:])
-                copy_words(
-                    half,
-                    grouped_words[:, 2 * half : 2 * half + 2],
-                    bank[:].rearrange("q t u p -> q t p u"),
+                        turn_words(bank[:, tt, u, :], words, (2 * half + tt) * WORDS + u * P)
+                copy = nc.scalar.copy if half == 0 else nc.vector.tensor_copy
+                copy(
+                    out=grouped_words[:, 2 * half : 2 * half + 2],
+                    in_=bank[:].rearrange("q t u p -> q t p u"),
                 )
             nc.vector.quantize_mx(out=codes.bitcast(FP8X4), scales=scales, in_=grouped[:])
 
-        def spread_bias(i):
-            cols = slice(i * D, (i + 1) * D)
-            bank = psum.tile([P, D], F32, name="tr_bank", tag="tr")
-            nc.tensor.matmul(out=bank[:], lhsT=ones[:], rhs=bias_rows[:, cols], start=True, stop=True)
-            nc.vector.tensor_copy(out=bias_bc[:, cols], in_=bank[:])
+        def spread_bias(rows, spread, copy):
+            bank = turn_banks.tile([P, D], F32, name="bias_bank", tag="turn")
+            nc.tensor.matmul(out=bank[:], lhsT=ones[:], rhs=rows, start=True, stop=True)
+            copy(out=spread, in_=bank[:])
 
         o_codes = [None] * B
         o_scales = [None] * B
         xb = [None] * B
+        x_loc = [None] * B
+        sums = [None] * B
+        normed = [None] * B
+        h_codes = [None] * B
+        h_scales = [None] * B
+        rstd = [None] * B
+        shift = [None] * B
 
         def prepare_o(b):
             words = o_sb[b][:].bitcast(F32)
-            bank = psum.tile([P, J, 2, P], F32, name="tr_bank", tag="tr")
+            bank = turn_banks.tile([P, J, 2, P], F32, name="o_bank", tag="turn")
             for j in range(J):
                 for u in range(2):
-                    start = j * WORDS + u * P
-                    nc.tensor.transpose(bank[:, j, u, :], words[:, start : start + P], ident[:])
+                    turn_words(bank[:, j, u, :], words, j * WORDS + u * P)
             grouped = stage.tile([P, J * D], BF16, align_bytes=64, name="grouped_o")
             nc.scalar.copy(
                 out=grouped[:].bitcast(F32).rearrange("q (j s u) -> q j s u", j=J, u=2),
@@ -135,22 +137,19 @@ def tile_block_pa_kernel(
             nc.vector.quantize_mx(
                 out=o_codes[b][:].bitcast(FP8X4), scales=o_scales[b][:], in_=grouped[:]
             )
-            xb[b] = stage.tile([P, J, D], F32, name="xb")
-            nc.gpsimd.tensor_tensor(
-                out=xb[b][:],
-                in0=x_sb[b][:].rearrange("p (j d) -> p j d", j=J),
-                in1=bo_bc.unsqueeze(1).to_broadcast([P, J, D]),
-                op=ALU.add,
-            )
 
-        x_loc = [None] * B
-        sums = [None] * B
+        def add_bias_to_x(b):
+            xb[b] = stage.tile([P, J, D], F32, name="xb")
+            for j in range(J):
+                nc.gpsimd.tensor_tensor(
+                    out=xb[b][:, j, :], in0=x_sb[b][:, j * D : (j + 1) * D], in1=bo_bc[:], op=ALU.add
+                )
 
         def first_product(b):
             x_loc[b] = results.tile([P, J, D], F32, name="x_loc")
-            sums[b] = stage.tile([P, J], F32, name="sums")
+            sums[b] = results.tile([P, J], F32, name="sums")
             for j in range(J):
-                acc = psum.tile([P, D], F32, name="acc1", tag="acc1")
+                acc = sum_banks.tile([P, D], F32, name="acc1", tag="acc")
                 nc.tensor.matmul_mx(
                     out=acc[:],
                     lhsT=o_codes[b][:, j * P : (j + 1) * P].bitcast(FP8X4),
@@ -174,7 +173,7 @@ def tile_block_pa_kernel(
                 in_=x_loc[b][:].rearrange("p j d -> p (j d)"),
             )
 
-        def normalise_and_quantise(b):
+        def statistics(b):
             neg_mean = stage.tile([P, J], F32, name="neg_mean")
             nc.scalar.mul(out=neg_mean[:], in_=sums[b][:], mul=-1.0 / D)
             sum_sq = stage.tile([P, J], F32, name="sum_sq")
@@ -188,61 +187,73 @@ def tile_block_pa_kernel(
                     scale=1.0,
                     accum_out=sum_sq[:, j : j + 1],
                 )
-            std = stage.tile([P, J], F32, name="std")
-            nc.scalar.activation(out=std[:], in_=sum_sq[:], func=ACT.Sqrt, bias=eps_col[:], scale=1.0 / D)
-            rstd = stage.tile([P, J], F32, name="rstd")
-            nc.vector.reciprocal(out=rstd[:], in_=std[:])
-            shift = stage.tile([P, J], F32, name="shift")
-            nc.vector.tensor_mul(out=shift[:], in0=neg_mean[:], in1=rstd[:])
-            normed = stage.tile([P, J, 2, WORDS], F32, name="normed")
+            rstd[b] = stage.tile([P, J], F32, name="rstd")
+            nc.scalar.activation(
+                out=rstd[b][:], in_=sum_sq[:], func=RSQRT, bias=eps_col[:], scale=1.0 / D
+            )
+            shift[b] = stage.tile([P, J], F32, name="shift")
             for j in range(J):
                 nc.scalar.activation(
-                    out=normed[:, j],
+                    out=shift[b][:, j : j + 1],
+                    in_=neg_mean[:, j : j + 1],
+                    func=ACT.Copy,
+                    scale=rstd[b][:, j : j + 1],
+                )
+
+        def normalise(b):
+            normed[b] = stage.tile([P, J, 2, WORDS], F32, name="normed")
+            for j in range(J):
+                nc.scalar.activation(
+                    out=normed[b][:, j],
                     in_=x_loc[b][:, j, :].rearrange("p (c e) -> p e c", e=2),
                     func=ACT.Identity,
-                    bias=shift[:, j : j + 1],
-                    scale=rstd[:, j : j + 1],
+                    bias=shift[b][:, j : j + 1],
+                    scale=rstd[b][:, j : j + 1],
                 )
+
+        def finish_h(b):
             h_t = stage.tile([P, 4, S], BF16, name="h_t")
+            banks = []
             for u in range(2):
-                bank = psum.tile([P, 2, S], F32, name="ht_bank", tag="ht")
+                bank = turn_banks.tile([P, 2, S], F32, name="h_bank", tag="turn")
+                banks.append(bank)
                 for e in range(2):
                     for j in range(J):
                         nc.tensor.transpose(
                             bank[:, e, j * P : (j + 1) * P],
-                            normed[:, j, e, u * P : (u + 1) * P],
+                            normed[b][:, j, e, u * P : (u + 1) * P],
                             ident[:],
                         )
+            for u in range(2):
                 for e in range(2):
                     t = 2 * u + e
                     nc.scalar.activation(
                         out=h_t[:, t, :],
-                        in_=bank[:, e, :],
+                        in_=banks[u][:, e, :],
                         func=ACT.Identity,
                         bias=ln_cols[:, 4 + t : 5 + t],
                         scale=ln_cols[:, t : t + 1],
                     )
             grouped = stage.tile([P, S, 4], BF16, align_bytes=64, name="grouped_h")
             nc.vector.tensor_copy(out=grouped[:], in_=h_t[:].rearrange("q t s -> q s t"))
-            h_codes = stage.tile([P, S], U32, align_bytes=64, name="h_codes")
-            h_scales = stage.tile([P, S], U8, align_bytes=64, name="h_scales")
+            h_codes[b] = stage.tile([P, S], U32, align_bytes=64, name="h_codes")
+            h_scales[b] = stage.tile([P, S], U8, align_bytes=64, name="h_scales")
             nc.vector.quantize_mx(
-                out=h_codes[:].bitcast(FP8X4),
-                scales=h_scales[:],
+                out=h_codes[b][:].bitcast(FP8X4),
+                scales=h_scales[b][:],
                 in_=grouped[:].rearrange("q s t -> q (s t)"),
             )
-            return h_codes, h_scales
 
-        def second_product(b, h_codes, h_scales):
+        def second_product(b):
             for c in range(N_QKV):
                 cols = slice(c * D, (c + 1) * D)
                 heads = results.tile([P, NH, J, HD], F32, name="heads")
                 for j in range(J):
-                    acc = psum.tile([P, D], F32, name="acc2", tag="acc2")
+                    acc = sum_banks.tile([P, D], F32, name="acc2", tag="acc")
                     nc.tensor.matmul_mx(
                         out=acc[:],
-                        lhsT=h_codes[:, j * P : (j + 1) * P].bitcast(FP8X4),
-                        lhsT_scale=h_scales[:, j * P : (j + 1) * P],
+                        lhsT=h_codes[b][:, j * P : (j + 1) * P].bitcast(FP8X4),
+                        lhsT_scale=h_scales[b][:, j * P : (j + 1) * P],
                         rhs=wqkv_codes[:, cols].bitcast(FP8X4),
                         rhs_scale=wqkv_scales[:, cols],
                         start=True,
@@ -259,33 +270,46 @@ def tile_block_pa_kernel(
                     in_=heads[:].rearrange("p n j d -> p n (j d)"),
                 )
 
-        eps_col = keep.tile([P, 1], F32)
-        nc.vector.memset(eps_col[:], EPS)
+        bo_bc = keep.tile([P, D], BF16)
+        bq_bc = keep.tile([P, N_QKV * D], BF16)
         wo_codes = keep.tile([P, D], U32, align_bytes=64)
         wo_scales = keep.tile([P, D], U8, align_bytes=64)
         wqkv_codes = keep.tile([P, N_QKV * D], U32, align_bytes=64)
         wqkv_scales = keep.tile([P, N_QKV * D], U8, align_bytes=64)
 
-        spread_bias(0)
-        prepare_o(0)
+        spread_bias(bo_rows[:], bo_bc[:], nc.vector.tensor_copy)
         quantise_weight(wo_sb, wo_codes[:], wo_scales[:])
+        prepare_o(0)
+        add_bias_to_x(0)
         first_product(0)
+        prepare_o(1)
+        add_bias_to_x(1)
 
-        ln_bank = psum.tile([P, P], F32, name="tr_bank", tag="tr")
+        ln_bank = turn_banks.tile([P, P], F32, name="ln_bank", tag="turn")
         nc.tensor.transpose(ln_bank[:], ln_rows[:].bitcast(F32), ident[:])
         ln_pairs = keep.tile([P, 8], BF16)
         nc.vector.tensor_copy(out=ln_pairs[:].bitcast(F32), in_=ln_bank[:, 0:4])
         ln_cols = keep.tile([P, 8], F32)
         nc.vector.tensor_copy(out=ln_cols[:], in_=ln_pairs[:])
 
-        for c in range(N_QKV):
-            spread_bias(1 + c)
-            cols = slice(c * D, (c + 1) * D)
-            quantise_weight(wqkv_sb[c], wqkv_codes[:, cols], wqkv_scales[:, cols])
-
-        for b in range(B):
-            if b + 1 < B:
-                prepare_o(b + 1)
-                first_product(b + 1)
-            h_codes, h_scales = normalise_and_quantise(b)
-            second_product(b, h_codes, h_scales)
+        for i in range(B + 1):
+            if i >= 1:
+                second_product(i - 1)
+            if i + 1 < B:
+                first_product(i + 1)
+            if i < B:
+                statistics(i)
+                normalise(i)
+            if i == 0:
+                for c in range(N_QKV):
+                    cols = slice(c * D, (c + 1) * D)
+                    quantise_weight(wqkv_sb[c], wqkv_codes[:, cols], wqkv_scales[:, cols])
+            if i < B:
+                finish_h(i)
+            if i == 0:
+                for c in range(N_QKV):
+                    cols = slice(c * D, (c + 1) * D)
+                    spread_bias(bq_rows[:, cols], bq_bc[:, cols], nc.scalar.copy)
+            if i + 2 < B:
+                prepare_o(i + 2)
+                add_bias_to_x(i + 2)

@@ -5,6 +5,7 @@ from concourse.masks import make_identity
 
 F32 = mybir.dt.float32
 BF16 = mybir.dt.bfloat16
+I32 = mybir.dt.int32
 U32 = mybir.dt.uint32
 U8 = mybir.dt.uint8
 FP8X4 = mybir.dt.float8_e4m3fn_x4
@@ -19,8 +20,11 @@ D = 512
 NH = 4
 HD = 128
 J = S // P
+TILES = B * J
+PACK = 4
 WORDS = D // 2
 N_QKV = 3
+PSUM_BANKS = 8
 EPS = 1e-5
 
 FLOPS = 2 * B * S * D * (D + N_QKV * D)
@@ -34,21 +38,22 @@ def tile_block_pa_kernel(
 
     with ExitStack() as stack:
         keep = stack.enter_context(tc.tile_pool(name="keep", bufs=1))
-        stage = stack.enter_context(tc.tile_pool(name="stage", bufs=2))
-        results = stack.enter_context(tc.tile_pool(name="results", bufs=4))
-        turn_banks = stack.enter_context(tc.psum_pool(name="turn_banks", bufs=3))
-        sum_banks = stack.enter_context(tc.psum_pool(name="sum_banks", bufs=5))
+        per_weight = stack.enter_context(tc.tile_pool(name="per_weight", bufs=1 + N_QKV))
+        per_batch = stack.enter_context(tc.tile_pool(name="per_batch", bufs=B))
+        per_tile = stack.enter_context(tc.tile_pool(name="per_tile", bufs=TILES))
+        results = stack.enter_context(tc.tile_pool(name="results", bufs=2 * N_QKV))
+        banks = stack.enter_context(tc.psum_pool(name="banks", bufs=PSUM_BANKS))
 
         bo_rows = keep.tile([P, D], BF16)
-        nc.vector.memset(bo_rows[:], 0.0)
+        nc.vector.memset(bo_rows[:].bitcast(I32), 0)
         ln_rows = keep.tile([P, 2 * P], BF16)
-        nc.vector.memset(ln_rows[:], 0.0)
+        nc.vector.memset(ln_rows[:].bitcast(I32), 0)
         eps_col = keep.tile([P, 1], F32)
         nc.vector.memset(eps_col[:], EPS)
+        bq_rows = keep.tile([P, N_QKV * D], BF16)
+        nc.vector.memset(bq_rows[:].bitcast(I32), 0)
         ones = keep.tile([P, P], BF16)
         nc.vector.memset(ones[:], 1.0)
-        bq_rows = keep.tile([P, N_QKV * D], BF16)
-        nc.vector.memset(bq_rows[:], 0.0)
         ident = keep.tile([P, P], F32)
         make_identity(nc, ident[:])
 
@@ -57,12 +62,14 @@ def tile_block_pa_kernel(
         wo_sb = keep.tile([P, 4 * D], BF16)
         wqkv_sb = [keep.tile([P, 4 * D], BF16, name="wqkv_sb%d" % c) for c in range(N_QKV)]
 
-        def load_o_and_x(b):
+        def load_o(b):
             for j in range(J):
                 nc.sync.dma_start(
                     out=o_sb[b][:, j * D : (j + 1) * D].rearrange("p (n d) -> p n d", n=NH),
                     in_=o_loc[b].rearrange("n (p j) d -> p j n d", j=J)[:, j],
                 )
+
+        def load_x(b):
             nc.sync.dma_start(out=x_sb[b][:], in_=x[b].rearrange("(p j) d -> p (j d)", j=J))
 
         def load_weight(w_sb, rows):
@@ -75,200 +82,235 @@ def tile_block_pa_kernel(
         nc.scalar.dma_start(out=ln_rows[0:2, :], in_=ln2_w.rearrange("(u c) -> u c", u=2))
         nc.scalar.dma_start(out=ln_rows[2:4, :], in_=ln2_b.rearrange("(u c) -> u c", u=2))
         nc.scalar.dma_start(out=bq_rows[0:1, :], in_=bqkv_g.rearrange("(o d) -> o d", o=1))
+        load_o(0)
         load_weight(wo_sb, Wo_l)
-        load_o_and_x(0)
-        load_o_and_x(1)
+        load_x(0)
+        load_o(1)
+        load_x(1)
         for c in range(N_QKV):
             load_weight(wqkv_sb[c], Wqkv_g[c * D : (c + 1) * D, :])
-        load_o_and_x(2)
-        load_o_and_x(3)
+        for b in range(2, B):
+            load_o(b)
+            load_x(b)
 
         warm = keep.tile([P, 1], F32)
         nc.scalar.activation(out=warm[:], in_=eps_col[:], func=RSQRT)
 
+        def new_bank(shape, name):
+            return banks.tile(shape, F32, name=name, tag="bank")
+
         def turn_words(bank, words, first_word):
             nc.tensor.transpose(bank, words[:, first_word : first_word + P], ident[:])
 
-        def quantise_weight(w_sb, codes, scales):
+        def spread_bias(rows):
+            bank = new_bank([P, D], "bias_bank")
+            nc.tensor.matmul(out=bank[:], lhsT=ones[:], rhs=rows, start=True, stop=True)
+            return bank
+
+        def turn_weight(w_sb):
             words = w_sb[:].bitcast(F32)
-            grouped = stage.tile([P, 4 * D], BF16, align_bytes=64, name="grouped_w")
-            grouped_words = grouped[:].bitcast(F32).rearrange("q (t p u) -> q t p u", t=4, u=2)
+            halves = []
             for half in range(2):
-                bank = turn_banks.tile([P, 2, 2, P], F32, name="w_bank", tag="turn")
+                bank = new_bank([P, 2, 2, P], "w_bank")
                 for tt in range(2):
                     for u in range(2):
                         turn_words(bank[:, tt, u, :], words, (2 * half + tt) * WORDS + u * P)
-                copy = nc.scalar.copy if half == 0 else nc.vector.tensor_copy
-                copy(
-                    out=grouped_words[:, 2 * half : 2 * half + 2],
-                    in_=bank[:].rearrange("q t u p -> q t p u"),
-                )
+                halves.append(bank)
+            return halves
+
+        def copy_weight_half(copy, halves, grouped, half):
+            grouped_words = grouped[:].bitcast(F32).rearrange("q (t p u) -> q t p u", t=4, u=2)
+            copy(
+                out=grouped_words[:, 2 * half : 2 * half + 2],
+                in_=halves[half][:].rearrange("q t u p -> q t p u"),
+            )
+
+        def new_grouped_weight():
+            return per_weight.tile([P, PACK * D], BF16, align_bytes=64, name="grouped_w")
+
+        def quantise_weight(grouped, codes, scales):
             nc.vector.quantize_mx(out=codes.bitcast(FP8X4), scales=scales, in_=grouped[:])
 
-        def spread_bias(rows, spread, copy):
-            bank = turn_banks.tile([P, D], F32, name="bias_bank", tag="turn")
-            nc.tensor.matmul(out=bank[:], lhsT=ones[:], rhs=rows, start=True, stop=True)
-            copy(out=spread, in_=bank[:])
-
+        o_bank = [None] * B
+        grouped_o = [None] * B
         o_codes = [None] * B
         o_scales = [None] * B
-        xb = [None] * B
-        x_loc = [None] * B
-        sums = [None] * B
-        normed = [None] * B
-        h_codes = [None] * B
-        h_scales = [None] * B
-        rstd = [None] * B
-        shift = [None] * B
 
-        def prepare_o(b):
+        def turn_o(b):
             words = o_sb[b][:].bitcast(F32)
-            bank = turn_banks.tile([P, J, 2, P], F32, name="o_bank", tag="turn")
+            o_bank[b] = new_bank([P, J, 2, P], "o_bank")
             for j in range(J):
                 for u in range(2):
-                    turn_words(bank[:, j, u, :], words, j * WORDS + u * P)
-            grouped = stage.tile([P, J * D], BF16, align_bytes=64, name="grouped_o")
+                    turn_words(o_bank[b][:, j, u, :], words, j * WORDS + u * P)
+
+        def copy_o(b):
+            grouped_o[b] = per_batch.tile([P, J * D], BF16, align_bytes=64, name="grouped_o")
             nc.scalar.copy(
-                out=grouped[:].bitcast(F32).rearrange("q (j s u) -> q j s u", j=J, u=2),
-                in_=bank[:].rearrange("q j u s -> q j s u"),
+                out=grouped_o[b][:].bitcast(F32).rearrange("q (j s u) -> q j s u", j=J, u=2),
+                in_=o_bank[b][:].rearrange("q j u s -> q j s u"),
             )
-            o_codes[b] = stage.tile([P, J * P], U32, align_bytes=64, name="o_codes")
-            o_scales[b] = stage.tile([P, J * P], U8, align_bytes=64, name="o_scales")
+
+        def quantise_o(b):
+            o_codes[b] = per_batch.tile([P, J * P], U32, align_bytes=64, name="o_codes")
+            o_scales[b] = per_batch.tile([P, J * P], U8, align_bytes=64, name="o_scales")
             nc.vector.quantize_mx(
-                out=o_codes[b][:].bitcast(FP8X4), scales=o_scales[b][:], in_=grouped[:]
+                out=o_codes[b][:].bitcast(FP8X4), scales=o_scales[b][:], in_=grouped_o[b][:]
             )
 
-        def add_bias_to_x(b):
-            xb[b] = stage.tile([P, J, D], F32, name="xb")
-            for j in range(J):
-                nc.gpsimd.tensor_tensor(
-                    out=xb[b][:, j, :], in0=x_sb[b][:, j * D : (j + 1) * D], in1=bo_bc[:], op=ALU.add
-                )
+        xb = [per_batch.tile([P, J, D], F32, name="xb") for b in range(B)]
+        x_loc = [per_batch.tile([P, J, D], F32, name="x_loc") for b in range(B)]
+        acc1 = [None] * TILES
+        sums = [None] * TILES
 
-        def first_product(b):
-            x_loc[b] = results.tile([P, J, D], F32, name="x_loc")
-            sums[b] = results.tile([P, J], F32, name="sums")
-            for j in range(J):
-                acc = sum_banks.tile([P, D], F32, name="acc1", tag="acc")
-                nc.tensor.matmul_mx(
-                    out=acc[:],
-                    lhsT=o_codes[b][:, j * P : (j + 1) * P].bitcast(FP8X4),
-                    lhsT_scale=o_scales[b][:, j * P : (j + 1) * P],
-                    rhs=wo_codes[:].bitcast(FP8X4),
-                    rhs_scale=wo_scales[:],
-                    start=True,
-                    stop=True,
-                )
-                nc.vector.scalar_tensor_tensor(
-                    out=x_loc[b][:, j, :],
-                    in0=acc[:],
-                    scalar=1.0,
-                    in1=xb[b][:, j, :],
-                    op0=ALU.mult,
-                    op1=ALU.add,
-                    accum_out=sums[b][:, j : j + 1],
-                )
-            nc.sync.dma_start(
-                out=out_0[b].rearrange("(p j) d -> p (j d)", j=J),
-                in_=x_loc[b][:].rearrange("p j d -> p (j d)"),
+        def add_bias_to_x(i):
+            b, j = divmod(i, J)
+            nc.gpsimd.tensor_tensor(
+                out=xb[b][:, j, :], in0=x_sb[b][:, j * D : (j + 1) * D], in1=bo_bc[:], op=ALU.add
             )
 
-        def statistics(b):
-            neg_mean = stage.tile([P, J], F32, name="neg_mean")
-            nc.scalar.mul(out=neg_mean[:], in_=sums[b][:], mul=-1.0 / D)
-            sum_sq = stage.tile([P, J], F32, name="sum_sq")
-            for j in range(J):
-                squares = stage.tile([P, D], BF16, name="squares")
-                nc.scalar.activation(
-                    out=squares[:],
-                    in_=x_loc[b][:, j, :],
-                    func=ACT.Square,
-                    bias=neg_mean[:, j : j + 1],
-                    scale=1.0,
-                    accum_out=sum_sq[:, j : j + 1],
+        def first_product(i):
+            b, j = divmod(i, J)
+            acc1[i] = new_bank([P, D], "acc1")
+            nc.tensor.matmul_mx(
+                out=acc1[i][:],
+                lhsT=o_codes[b][:, j * P : (j + 1) * P].bitcast(FP8X4),
+                lhsT_scale=o_scales[b][:, j * P : (j + 1) * P],
+                rhs=wo_codes[:].bitcast(FP8X4),
+                rhs_scale=wo_scales[:],
+                start=True,
+                stop=True,
+            )
+
+        def add_residual(i):
+            b, j = divmod(i, J)
+            sums[i] = per_tile.tile([P, 1], F32, name="sums")
+            nc.vector.scalar_tensor_tensor(
+                out=x_loc[b][:, j, :],
+                in0=acc1[i][:],
+                scalar=1.0,
+                in1=xb[b][:, j, :],
+                op0=ALU.mult,
+                op1=ALU.add,
+                accum_out=sums[i][:],
+            )
+            if j == J - 1:
+                nc.sync.dma_start(
+                    out=out_0[b].rearrange("(p j) d -> p (j d)", j=J),
+                    in_=x_loc[b][:].rearrange("p j d -> p (j d)"),
                 )
-            rstd[b] = stage.tile([P, J], F32, name="rstd")
+
+        normed = [None] * TILES
+        h_bank = [None] * TILES
+        h_t = [None] * TILES
+        grouped_h = [None] * TILES
+        h_codes = [None] * TILES
+        h_scales = [None] * TILES
+
+        def layer_norm(i, between):
+            b, j = divmod(i, J)
+            neg_mean = per_tile.tile([P, 1], F32, name="neg_mean")
+            nc.scalar.mul(out=neg_mean[:], in_=sums[i][:], mul=-1.0 / D)
+            between[0]()
+            squares = per_tile.tile([P, D], BF16, name="squares")
+            sum_sq = per_tile.tile([P, 1], F32, name="sum_sq")
             nc.scalar.activation(
-                out=rstd[b][:], in_=sum_sq[:], func=RSQRT, bias=eps_col[:], scale=1.0 / D
+                out=squares[:],
+                in_=x_loc[b][:, j, :],
+                func=ACT.Square,
+                bias=neg_mean[:],
+                scale=1.0,
+                accum_out=sum_sq[:],
             )
-            shift[b] = stage.tile([P, J], F32, name="shift")
-            for j in range(J):
-                nc.scalar.activation(
-                    out=shift[b][:, j : j + 1],
-                    in_=neg_mean[:, j : j + 1],
-                    func=ACT.Copy,
-                    scale=rstd[b][:, j : j + 1],
-                )
+            between[1]()
+            rstd = per_tile.tile([P, 1], F32, name="rstd")
+            nc.scalar.activation(
+                out=rstd[:], in_=sum_sq[:], func=RSQRT, bias=eps_col[:], scale=1.0 / D
+            )
+            between[2]()
+            shift = per_tile.tile([P, 1], F32, name="shift")
+            nc.scalar.activation(out=shift[:], in_=neg_mean[:], func=ACT.Copy, scale=rstd[:])
+            between[3]()
+            normed[i] = per_tile.tile([P, 2, WORDS], F32, name="normed")
+            nc.scalar.activation(
+                out=normed[i][:],
+                in_=x_loc[b][:, j, :].rearrange("p (c e) -> p e c", e=2),
+                func=ACT.Identity,
+                bias=shift[:],
+                scale=rstd[:],
+            )
 
-        def normalise(b):
-            normed[b] = stage.tile([P, J, 2, WORDS], F32, name="normed")
-            for j in range(J):
-                nc.scalar.activation(
-                    out=normed[b][:, j],
-                    in_=x_loc[b][:, j, :].rearrange("p (c e) -> p e c", e=2),
-                    func=ACT.Identity,
-                    bias=shift[b][:, j : j + 1],
-                    scale=rstd[b][:, j : j + 1],
-                )
-
-        def finish_h(b):
-            h_t = stage.tile([P, 4, S], BF16, name="h_t")
-            banks = []
-            for u in range(2):
-                bank = turn_banks.tile([P, 2, S], F32, name="h_bank", tag="turn")
-                banks.append(bank)
-                for e in range(2):
-                    for j in range(J):
-                        nc.tensor.transpose(
-                            bank[:, e, j * P : (j + 1) * P],
-                            normed[b][:, j, e, u * P : (u + 1) * P],
-                            ident[:],
-                        )
+        def turn_h(i):
+            h_bank[i] = new_bank([P, PACK, P], "h_bank")
             for u in range(2):
                 for e in range(2):
-                    t = 2 * u + e
-                    nc.scalar.activation(
-                        out=h_t[:, t, :],
-                        in_=banks[u][:, e, :],
-                        func=ACT.Identity,
-                        bias=ln_cols[:, 4 + t : 5 + t],
-                        scale=ln_cols[:, t : t + 1],
+                    nc.tensor.transpose(
+                        h_bank[i][:, 2 * u + e, :], normed[i][:, e, u * P : (u + 1) * P], ident[:]
                     )
-            grouped = stage.tile([P, S, 4], BF16, align_bytes=64, name="grouped_h")
-            nc.vector.tensor_copy(out=grouped[:], in_=h_t[:].rearrange("q t s -> q s t"))
-            h_codes[b] = stage.tile([P, S], U32, align_bytes=64, name="h_codes")
-            h_scales[b] = stage.tile([P, S], U8, align_bytes=64, name="h_scales")
+            h_t[i] = per_tile.tile([P, PACK, P], BF16, name="h_t")
+
+        def gain_and_bias(i, t):
+            nc.scalar.activation(
+                out=h_t[i][:, t, :],
+                in_=h_bank[i][:, t, :],
+                func=ACT.Identity,
+                bias=ln_cols[:, PACK + t : PACK + t + 1],
+                scale=ln_cols[:, t : t + 1],
+            )
+
+        def gain_and_bias_calls(i):
+            return [lambda t=t: gain_and_bias(i, t) for t in range(PACK)]
+
+        def regroup_h(i):
+            grouped_h[i] = per_tile.tile([P, P, PACK], BF16, align_bytes=64, name="grouped_h")
+            nc.vector.tensor_copy(
+                out=grouped_h[i][:].rearrange("q (c r) t -> q c t r", r=4),
+                in_=h_t[i][:].rearrange("q t (c r) -> q c t r", r=4),
+            )
+
+        def quantise_h(i):
+            h_codes[i] = per_tile.tile([P, P], U32, align_bytes=64, name="h_codes")
+            h_scales[i] = per_tile.tile([P, P], U8, align_bytes=64, name="h_scales")
             nc.vector.quantize_mx(
-                out=h_codes[b][:].bitcast(FP8X4),
-                scales=h_scales[b][:],
-                in_=grouped[:].rearrange("q s t -> q (s t)"),
+                out=h_codes[i][:].bitcast(FP8X4),
+                scales=h_scales[i][:],
+                in_=grouped_h[i][:].rearrange("q s t -> q (s t)"),
             )
 
-        def second_product(b):
-            for c in range(N_QKV):
-                cols = slice(c * D, (c + 1) * D)
-                heads = results.tile([P, NH, J, HD], F32, name="heads")
-                for j in range(J):
-                    acc = sum_banks.tile([P, D], F32, name="acc2", tag="acc")
-                    nc.tensor.matmul_mx(
-                        out=acc[:],
-                        lhsT=h_codes[b][:, j * P : (j + 1) * P].bitcast(FP8X4),
-                        lhsT_scale=h_scales[b][:, j * P : (j + 1) * P],
-                        rhs=wqkv_codes[:, cols].bitcast(FP8X4),
-                        rhs_scale=wqkv_scales[:, cols],
-                        start=True,
-                        stop=True,
-                    )
-                    nc.vector.tensor_tensor(
-                        out=heads[:, :, j, :],
-                        in0=acc[:].rearrange("p (n d) -> p n d", n=NH),
-                        in1=bq_bc[:, cols].rearrange("p (n d) -> p n d", n=NH),
-                        op=ALU.add,
-                    )
+        acc2 = {}
+        heads = {}
+
+        def second_product(i, c):
+            cols = slice(c * D, (c + 1) * D)
+            acc2[i, c] = new_bank([P, D], "acc2")
+            nc.tensor.matmul_mx(
+                out=acc2[i, c][:],
+                lhsT=h_codes[i][:].bitcast(FP8X4),
+                lhsT_scale=h_scales[i][:],
+                rhs=wqkv_codes[:, cols].bitcast(FP8X4),
+                rhs_scale=wqkv_scales[:, cols],
+                start=True,
+                stop=True,
+            )
+
+        def add_bias(i, c):
+            b, j = divmod(i, J)
+            cols = slice(c * D, (c + 1) * D)
+            if j == 0:
+                heads[b, c] = results.tile([P, NH, J, HD], F32, name="heads")
+            nc.vector.tensor_tensor(
+                out=heads[b, c][:, :, j, :],
+                in0=acc2[i, c][:].rearrange("p (n d) -> p n d", n=NH),
+                in1=bq_bc[:, cols].rearrange("p (n d) -> p n d", n=NH),
+                op=ALU.add,
+            )
+            if j == J - 1:
                 nc.sync.dma_start(
                     out=qkv_out[c][b].rearrange("n (p j) d -> p n (j d)", j=J),
-                    in_=heads[:].rearrange("p n j d -> p n (j d)"),
+                    in_=heads[b, c][:].rearrange("p n j d -> p n (j d)"),
                 )
+
+        def nothing():
+            return None
 
         bo_bc = keep.tile([P, D], BF16)
         bq_bc = keep.tile([P, N_QKV * D], BF16)
@@ -276,40 +318,118 @@ def tile_block_pa_kernel(
         wo_scales = keep.tile([P, D], U8, align_bytes=64)
         wqkv_codes = keep.tile([P, N_QKV * D], U32, align_bytes=64)
         wqkv_scales = keep.tile([P, N_QKV * D], U8, align_bytes=64)
+        qkv_cols = [slice(c * D, (c + 1) * D) for c in range(N_QKV)]
 
-        spread_bias(bo_rows[:], bo_bc[:], nc.vector.tensor_copy)
-        quantise_weight(wo_sb, wo_codes[:], wo_scales[:])
-        prepare_o(0)
-        add_bias_to_x(0)
-        first_product(0)
-        prepare_o(1)
-        add_bias_to_x(1)
+        turn_o(0)
+        copy_o(0)
+        quantise_o(0)
+        bo_bank = spread_bias(bo_rows[:])
+        nc.vector.tensor_copy(out=bo_bc[:], in_=bo_bank[:])
 
-        ln_bank = turn_banks.tile([P, P], F32, name="ln_bank", tag="turn")
+        ln_bank = new_bank([P, P], "ln_bank")
         nc.tensor.transpose(ln_bank[:], ln_rows[:].bitcast(F32), ident[:])
-        ln_pairs = keep.tile([P, 8], BF16)
-        nc.vector.tensor_copy(out=ln_pairs[:].bitcast(F32), in_=ln_bank[:, 0:4])
-        ln_cols = keep.tile([P, 8], F32)
+        ln_pairs = keep.tile([P, 2 * PACK], BF16)
+        nc.vector.tensor_copy(out=ln_pairs[:].bitcast(F32), in_=ln_bank[:, 0:PACK])
+        ln_cols = keep.tile([P, 2 * PACK], F32)
         nc.vector.tensor_copy(out=ln_cols[:], in_=ln_pairs[:])
 
-        for i in range(B + 1):
-            if i >= 1:
-                second_product(i - 1)
-            if i + 1 < B:
-                first_product(i + 1)
-            if i < B:
-                statistics(i)
-                normalise(i)
-            if i == 0:
-                for c in range(N_QKV):
-                    cols = slice(c * D, (c + 1) * D)
-                    quantise_weight(wqkv_sb[c], wqkv_codes[:, cols], wqkv_scales[:, cols])
-            if i < B:
-                finish_h(i)
-            if i == 0:
-                for c in range(N_QKV):
-                    cols = slice(c * D, (c + 1) * D)
-                    spread_bias(bq_rows[:, cols], bq_bc[:, cols], nc.scalar.copy)
-            if i + 2 < B:
-                prepare_o(i + 2)
-                add_bias_to_x(i + 2)
+        wo_halves = turn_weight(wo_sb)
+        grouped_wo = new_grouped_weight()
+        copy_weight_half(nc.scalar.copy, wo_halves, grouped_wo, 0)
+        copy_weight_half(nc.vector.tensor_copy, wo_halves, grouped_wo, 1)
+        quantise_weight(grouped_wo, wo_codes[:], wo_scales[:])
+
+        bq_banks = [spread_bias(bq_rows[:, cols]) for cols in qkv_cols]
+        nc.scalar.copy(out=bq_bc[:, qkv_cols[0]], in_=bq_banks[0][:])
+        nc.scalar.copy(out=bq_bc[:, qkv_cols[1]], in_=bq_banks[1][:])
+        nc.vector.tensor_copy(out=bq_bc[:, qkv_cols[2]], in_=bq_banks[2][:])
+
+        turn_o(1)
+        copy_o(1)
+        quantise_o(1)
+        for i in range(TILES):
+            add_bias_to_x(i)
+        for i in range(2 * J):
+            first_product(i)
+        for i in range(2 * J):
+            add_residual(i)
+
+        w_halves = [turn_weight(wqkv_sb[c]) for c in range(N_QKV)]
+        grouped_w = [new_grouped_weight() for c in range(N_QKV)]
+        turn_o(2)
+        layer_norm(
+            0,
+            [
+                nothing,
+                lambda: copy_weight_half(nc.scalar.copy, w_halves[0], grouped_w[0], 0),
+                lambda: copy_weight_half(nc.scalar.copy, w_halves[1], grouped_w[1], 0),
+                nothing,
+            ],
+        )
+        turn_h(0)
+        for c in range(2):
+            copy_weight_half(nc.vector.tensor_copy, w_halves[c], grouped_w[c], 1)
+        for c in range(2):
+            quantise_weight(grouped_w[c], wqkv_codes[:, qkv_cols[c]], wqkv_scales[:, qkv_cols[c]])
+        turn_o(3)
+        layer_norm(1, gain_and_bias_calls(0))
+        turn_h(1)
+        copy_weight_half(nc.scalar.copy, w_halves[2], grouped_w[2], 0)
+        copy_o(2)
+        copy_weight_half(nc.vector.tensor_copy, w_halves[2], grouped_w[2], 1)
+        regroup_h(0)
+        quantise_weight(grouped_w[2], wqkv_codes[:, qkv_cols[2]], wqkv_scales[:, qkv_cols[2]])
+        quantise_h(0)
+        quantise_o(2)
+        for i in range(2 * J, 3 * J):
+            first_product(i)
+        for i in range(2 * J, 3 * J):
+            add_residual(i)
+        layer_norm(2, gain_and_bias_calls(1))
+        turn_h(2)
+        copy_o(3)
+        regroup_h(1)
+        quantise_o(3)
+        quantise_h(1)
+        for i in range(3 * J, 4 * J):
+            first_product(i)
+        for i in range(3 * J, 4 * J):
+            add_residual(i)
+
+        def scalar_step(i):
+            if i < TILES:
+                layer_norm(i, gain_and_bias_calls(i - 1))
+                turn_h(i)
+            elif i - 1 < TILES:
+                for call in gain_and_bias_calls(i - 1):
+                    call()
+
+        for b in range(B):
+            i0 = J * b
+            i1 = i0 + 1
+            more = b + 1 < B
+
+            second_product(i0, 0)
+            second_product(i1, 0)
+            scalar_step(i0 + 3)
+            add_bias(i0, 0)
+            add_bias(i1, 0)
+            if more:
+                regroup_h(i0 + 2)
+
+            second_product(i0, 1)
+            second_product(i1, 1)
+            add_bias(i0, 1)
+            if more:
+                quantise_h(i0 + 2)
+            add_bias(i1, 1)
+            scalar_step(i0 + 4)
+            if more:
+                regroup_h(i0 + 3)
+
+            second_product(i0, 2)
+            second_product(i1, 2)
+            add_bias(i0, 2)
+            if more:
+                quantise_h(i0 + 3)
+            add_bias(i1, 2)

@@ -357,26 +357,19 @@ def tile_block_pa_kernel(
         w_halves = [turn_weight(wqkv_sb[c]) for c in range(N_QKV)]
         grouped_w = [new_grouped_weight() for c in range(N_QKV)]
         turn_o(2)
-        layer_norm(
-            0,
-            [
-                nothing,
-                lambda: copy_weight_half(nc.scalar.copy, w_halves[0], grouped_w[0], 0),
-                lambda: copy_weight_half(nc.scalar.copy, w_halves[1], grouped_w[1], 0),
-                nothing,
-            ],
-        )
+        layer_norm(0, [nothing] * PACK)
         turn_h(0)
         for c in range(2):
-            copy_weight_half(nc.vector.tensor_copy, w_halves[c], grouped_w[c], 1)
+            for half in range(2):
+                copy_weight_half(nc.vector.tensor_copy, w_halves[c], grouped_w[c], half)
         for c in range(2):
             quantise_weight(grouped_w[c], wqkv_codes[:, qkv_cols[c]], wqkv_scales[:, qkv_cols[c]])
         turn_o(3)
         layer_norm(1, gain_and_bias_calls(0))
         turn_h(1)
-        copy_weight_half(nc.scalar.copy, w_halves[2], grouped_w[2], 0)
         copy_o(2)
-        copy_weight_half(nc.vector.tensor_copy, w_halves[2], grouped_w[2], 1)
+        for half in range(2):
+            copy_weight_half(nc.vector.tensor_copy, w_halves[2], grouped_w[2], half)
         regroup_h(0)
         quantise_weight(grouped_w[2], wqkv_codes[:, qkv_cols[2]], wqkv_scales[:, qkv_cols[2]])
         quantise_h(0)

@@ -20,7 +20,6 @@ D = 512
 NH = 4
 HD = 128
 J = S // P
-TILES = B * J
 PACK = 4
 WORDS = D // 2
 N_QKV = 3
@@ -40,22 +39,22 @@ def tile_block_pa_kernel(
         keep = stack.enter_context(tc.tile_pool(name="keep", bufs=1))
         per_weight = stack.enter_context(tc.tile_pool(name="per_weight", bufs=1 + N_QKV))
         per_batch = stack.enter_context(tc.tile_pool(name="per_batch", bufs=B))
-        per_tile = stack.enter_context(tc.tile_pool(name="per_tile", bufs=TILES))
+        per_tile = stack.enter_context(tc.tile_pool(name="per_tile", bufs=B * J))
         results = stack.enter_context(tc.tile_pool(name="results", bufs=2 * N_QKV))
         banks = stack.enter_context(tc.psum_pool(name="banks", bufs=PSUM_BANKS))
+        stack.enter_context(tc.manual_schedule())
 
-        bo_rows = keep.tile([P, D], BF16)
-        nc.vector.memset(bo_rows[:].bitcast(I32), 0)
+        bias_rows = keep.tile([P, (N_QKV + 1) * D], BF16)
+        nc.vector.memset(bias_rows[:, N_QKV * D :].bitcast(I32), 0)
         ln_rows = keep.tile([P, 2 * P], BF16)
         nc.vector.memset(ln_rows[:].bitcast(I32), 0)
+        nc.vector.memset(bias_rows[:, 0 : N_QKV * D].bitcast(I32), 0)
         eps_col = keep.tile([P, 1], F32)
         nc.vector.memset(eps_col[:], EPS)
-        bq_rows = keep.tile([P, N_QKV * D], BF16)
-        nc.vector.memset(bq_rows[:].bitcast(I32), 0)
         ones = keep.tile([P, P], BF16)
         nc.vector.memset(ones[:], 1.0)
         ident = keep.tile([P, P], F32)
-        make_identity(nc, ident[:])
+        ident_bf = keep.tile([P, P], BF16)
 
         o_sb = [keep.tile([P, J * D], BF16, name="o_sb%d" % b) for b in range(B)]
         x_sb = [keep.tile([P, J * D], BF16, name="x_sb%d" % b) for b in range(B)]
@@ -78,58 +77,71 @@ def tile_block_pa_kernel(
                 in_=rows.rearrange("(t p) k -> p t k", p=P),
             )
 
-        nc.scalar.dma_start(out=bo_rows[0:1, :], in_=bo_l.rearrange("(o d) -> o d", o=1))
-        nc.scalar.dma_start(out=ln_rows[0:2, :], in_=ln2_w.rearrange("(u c) -> u c", u=2))
-        nc.scalar.dma_start(out=ln_rows[2:4, :], in_=ln2_b.rearrange("(u c) -> u c", u=2))
-        nc.scalar.dma_start(out=bq_rows[0:1, :], in_=bqkv_g.rearrange("(o d) -> o d", o=1))
+        def load_weight_half(w_sb, rows, half):
+            nc.sync.dma_start(
+                out=w_sb[:, half * 2 * D : (half + 1) * 2 * D].rearrange("p (t k) -> p t k", k=D),
+                in_=rows[half * 2 * P : (half + 1) * 2 * P, :].rearrange("(t p) k -> p t k", p=P),
+            )
+
+        bo_cols = slice(N_QKV * D, (N_QKV + 1) * D)
+        make_identity(nc, ident[:])
+        nc.scalar.dma_start(
+            out=bias_rows[0:1, bo_cols], in_=bo_l.rearrange("(o d) -> o d", o=1)
+        )
+        nc.gpsimd.dma_start(out=ln_rows[0:2, :], in_=ln2_w.rearrange("(u c) -> u c", u=2))
+        nc.gpsimd.dma_start(out=ln_rows[2:4, :], in_=ln2_b.rearrange("(u c) -> u c", u=2))
+        nc.gpsimd.dma_start(
+            out=bias_rows[0:1, 0 : N_QKV * D], in_=bqkv_g.rearrange("(o d) -> o d", o=1)
+        )
         load_o(0)
-        load_weight(wo_sb, Wo_l)
+        for half in range(2):
+            load_weight_half(wo_sb, Wo_l, half)
         load_x(0)
+        load_weight(wqkv_sb[0], Wqkv_g[0:D, :])
         load_o(1)
         load_x(1)
-        for c in range(N_QKV):
-            load_weight(wqkv_sb[c], Wqkv_g[c * D : (c + 1) * D, :])
+        load_weight(wqkv_sb[1], Wqkv_g[D : 2 * D, :])
+        load_weight(wqkv_sb[2], Wqkv_g[2 * D : 3 * D, :])
         for b in range(2, B):
             load_o(b)
             load_x(b)
 
+        nc.vector.tensor_copy(out=ident_bf[:], in_=ident[:])
+
         warm = keep.tile([P, 1], F32)
         nc.scalar.activation(out=warm[:], in_=eps_col[:], func=RSQRT)
 
-        def new_bank(shape, name):
-            return banks.tile(shape, F32, name=name, tag="bank")
+        def new_bank(shape, name, dtype=F32):
+            return banks.tile(shape, dtype, name=name, tag="bank")
 
         def turn_words(bank, words, first_word):
             nc.tensor.transpose(bank, words[:, first_word : first_word + P], ident[:])
 
-        def spread_bias(rows):
-            bank = new_bank([P, D], "bias_bank")
-            nc.tensor.matmul(out=bank[:], lhsT=ones[:], rhs=rows, start=True, stop=True)
-            return bank
+        w_bank = {}
+        grouped_w = {}
 
-        def turn_weight(w_sb):
+        def turn_weight(c, w_sb):
             words = w_sb[:].bitcast(F32)
-            halves = []
+            grouped_w[c] = per_weight.tile([P, PACK * D], BF16, align_bytes=64, name="grouped_w")
             for half in range(2):
-                bank = new_bank([P, 2, 2, P], "w_bank")
+                w_bank[c, half] = new_bank([P, 2, 2, P], "w_bank")
                 for tt in range(2):
                     for u in range(2):
-                        turn_words(bank[:, tt, u, :], words, (2 * half + tt) * WORDS + u * P)
-                halves.append(bank)
-            return halves
+                        turn_words(
+                            w_bank[c, half][:, tt, u, :], words, (2 * half + tt) * WORDS + u * P
+                        )
 
-        def copy_weight_half(copy, halves, grouped, half):
-            grouped_words = grouped[:].bitcast(F32).rearrange("q (t p u) -> q t p u", t=4, u=2)
+        def copy_weight(copy, c, half):
+            grouped_words = grouped_w[c][:].bitcast(F32).rearrange(
+                "q (t p u) -> q t p u", t=4, u=2
+            )
             copy(
                 out=grouped_words[:, 2 * half : 2 * half + 2],
-                in_=halves[half][:].rearrange("q t u p -> q t p u"),
+                in_=w_bank[c, half][:].rearrange("q t u p -> q t p u"),
             )
 
-        def new_grouped_weight():
-            return per_weight.tile([P, PACK * D], BF16, align_bytes=64, name="grouped_w")
-
-        def quantise_weight(grouped, codes, scales):
-            nc.vector.quantize_mx(out=codes.bitcast(FP8X4), scales=scales, in_=grouped[:])
+        def quantise_weight(c, codes, scales):
+            nc.vector.quantize_mx(out=codes.bitcast(FP8X4), scales=scales, in_=grouped_w[c][:])
 
         o_bank = [None] * B
         grouped_o = [None] * B
@@ -159,39 +171,57 @@ def tile_block_pa_kernel(
 
         xb = [per_batch.tile([P, J, D], F32, name="xb") for b in range(B)]
         x_loc = [per_batch.tile([P, J, D], F32, name="x_loc") for b in range(B)]
-        acc1 = [None] * TILES
-        sums = [None] * TILES
+        sums = [per_batch.tile([P, J], F32, name="sums") for b in range(B)]
+        acc1 = {}
 
-        def add_bias_to_x(i):
-            b, j = divmod(i, J)
-            nc.gpsimd.tensor_tensor(
-                out=xb[b][:, j, :], in0=x_sb[b][:, j * D : (j + 1) * D], in1=bo_bc[:], op=ALU.add
+        def add_bias_to_x(engine, b, j):
+            engine.tensor_tensor(
+                out=xb[b][:, j, :],
+                in0=x_sb[b][:, j * D : (j + 1) * D],
+                in1=bias_bc[:, bo_cols],
+                op=ALU.add,
             )
 
-        def first_product(i):
-            b, j = divmod(i, J)
-            acc1[i] = new_bank([P, D], "acc1")
-            nc.tensor.matmul_mx(
-                out=acc1[i][:],
-                lhsT=o_codes[b][:, j * P : (j + 1) * P].bitcast(FP8X4),
-                lhsT_scale=o_scales[b][:, j * P : (j + 1) * P],
-                rhs=wo_codes[:].bitcast(FP8X4),
-                rhs_scale=wo_scales[:],
+        x_bank = {}
+
+        def sum_bias_and_x(b, j):
+            x_bank[b, j] = new_bank([P, D], "x_bank")
+            nc.tensor.matmul(
+                out=x_bank[b, j][:],
+                lhsT=ident_bf[:],
+                rhs=x_sb[b][:, j * D : (j + 1) * D],
                 start=True,
-                stop=True,
+                stop=False,
+            )
+            nc.tensor.matmul(
+                out=x_bank[b, j][:], lhsT=ones[:], rhs=bias_rows[:, bo_cols], start=False, stop=True
             )
 
-        def add_residual(i):
-            b, j = divmod(i, J)
-            sums[i] = per_tile.tile([P, 1], F32, name="sums")
+        def copy_bias_and_x(b, j):
+            nc.scalar.copy(out=xb[b][:, j, :], in_=x_bank[b, j][:])
+
+        def first_product(b):
+            for j in range(J):
+                acc1[b, j] = new_bank([P, D], "acc1")
+                nc.tensor.matmul_mx(
+                    out=acc1[b, j][:],
+                    lhsT=o_codes[b][:, j * P : (j + 1) * P].bitcast(FP8X4),
+                    lhsT_scale=o_scales[b][:, j * P : (j + 1) * P],
+                    rhs=wo_codes[:].bitcast(FP8X4),
+                    rhs_scale=wo_scales[:],
+                    start=True,
+                    stop=True,
+                )
+
+        def add_residual(b, j):
             nc.vector.scalar_tensor_tensor(
                 out=x_loc[b][:, j, :],
-                in0=acc1[i][:],
+                in0=acc1[b, j][:],
                 scalar=1.0,
                 in1=xb[b][:, j, :],
                 op0=ALU.mult,
                 op1=ALU.add,
-                accum_out=sums[i][:],
+                accum_out=sums[b][:, j : j + 1],
             )
             if j == J - 1:
                 nc.sync.dma_start(
@@ -199,108 +229,189 @@ def tile_block_pa_kernel(
                     in_=x_loc[b][:].rearrange("p j d -> p (j d)"),
                 )
 
-        normed = [None] * TILES
-        h_bank = [None] * TILES
-        h_t = [None] * TILES
-        grouped_h = [None] * TILES
-        h_codes = [None] * TILES
-        h_scales = [None] * TILES
+        neg_mean = [None] * B
+        sum_sq = [None] * B
+        rstd = [None] * B
+        shift = [None] * B
+        normed = {}
+        h_bank = {}
+        h_t = [None] * B
+        grouped_h = [None] * B
+        h_codes = [None] * B
+        h_scales = [None] * B
 
-        def layer_norm(i, between):
-            b, j = divmod(i, J)
-            neg_mean = per_tile.tile([P, 1], F32, name="neg_mean")
-            nc.scalar.mul(out=neg_mean[:], in_=sums[i][:], mul=-1.0 / D)
-            between[0]()
+        def mean(b, j):
+            if j == 0:
+                neg_mean[b] = per_batch.tile([P, J], F32, name="neg_mean")
+                sum_sq[b] = per_batch.tile([P, J], F32, name="sum_sq")
+                shift[b] = per_batch.tile([P, J], F32, name="shift")
+            nc.scalar.mul(
+                out=neg_mean[b][:, j : j + 1], in_=sums[b][:, j : j + 1], mul=-1.0 / D
+            )
+
+        def deviations(b, j):
             squares = per_tile.tile([P, D], BF16, name="squares")
-            sum_sq = per_tile.tile([P, 1], F32, name="sum_sq")
             nc.scalar.activation(
                 out=squares[:],
                 in_=x_loc[b][:, j, :],
                 func=ACT.Square,
-                bias=neg_mean[:],
+                bias=neg_mean[b][:, j : j + 1],
                 scale=1.0,
-                accum_out=sum_sq[:],
-            )
-            between[1]()
-            rstd = per_tile.tile([P, 1], F32, name="rstd")
-            nc.scalar.activation(
-                out=rstd[:], in_=sum_sq[:], func=RSQRT, bias=eps_col[:], scale=1.0 / D
-            )
-            between[2]()
-            shift = per_tile.tile([P, 1], F32, name="shift")
-            nc.scalar.activation(out=shift[:], in_=neg_mean[:], func=ACT.Copy, scale=rstd[:])
-            between[3]()
-            normed[i] = per_tile.tile([P, 2, WORDS], F32, name="normed")
-            nc.scalar.activation(
-                out=normed[i][:],
-                in_=x_loc[b][:, j, :].rearrange("p (c e) -> p e c", e=2),
-                func=ACT.Identity,
-                bias=shift[:],
-                scale=rstd[:],
+                accum_out=sum_sq[b][:, j : j + 1],
             )
 
-        def turn_h(i):
-            h_bank[i] = new_bank([P, PACK, P], "h_bank")
+        def inverse_deviation(b, first=0, count=J):
+            if first == 0:
+                rstd[b] = per_batch.tile([P, J], F32, name="rstd")
+            nc.scalar.activation(
+                out=rstd[b][:, first : first + count],
+                in_=sum_sq[b][:, first : first + count],
+                func=RSQRT,
+                bias=eps_col[:],
+                scale=1.0 / D,
+            )
+
+        def shift_tile(b, j):
+            nc.scalar.activation(
+                out=shift[b][:, j : j + 1],
+                in_=neg_mean[b][:, j : j + 1],
+                func=ACT.Copy,
+                scale=rstd[b][:, j : j + 1],
+            )
+
+        def shifts(b):
+            for j in range(J):
+                shift_tile(b, j)
+
+        def normalise(b, j):
+            normed[b, j] = per_tile.tile([P, 2, WORDS], F32, name="normed")
+            nc.scalar.activation(
+                out=normed[b, j][:],
+                in_=x_loc[b][:, j, :].rearrange("p (c e) -> p e c", e=2),
+                func=ACT.Identity,
+                bias=shift[b][:, j : j + 1],
+                scale=rstd[b][:, j : j + 1],
+            )
+
+        def normalise_on_vector(b, j):
+            normed[b, j] = per_tile.tile([P, 2, WORDS], F32, name="normed")
+            nc.vector.tensor_scalar(
+                out=normed[b, j][:],
+                in0=x_loc[b][:, j, :].rearrange("p (c e) -> p e c", e=2),
+                scalar1=neg_mean[b][:, j : j + 1],
+                scalar2=rstd[b][:, j : j + 1],
+                op0=ALU.add,
+                op1=ALU.mult,
+            )
+
+        def turn_h(b):
+            for u in range(2):
+                h_bank[b, u] = new_bank([P, 2, J, P], "h_bank")
+            for j in range(J):
+                for u in range(2):
+                    for e in range(2):
+                        nc.tensor.transpose(
+                            h_bank[b, u][:, e, j, :],
+                            normed[b, j][:, e, u * P : (u + 1) * P],
+                            ident[:],
+                        )
+            h_t[b] = per_batch.tile([P, PACK, J * P], BF16, name="h_t")
+
+        def turn_h_tile(b, j):
+            h_bank[b, j] = new_bank([P, PACK, P], "h_bank")
             for u in range(2):
                 for e in range(2):
                     nc.tensor.transpose(
-                        h_bank[i][:, 2 * u + e, :], normed[i][:, e, u * P : (u + 1) * P], ident[:]
+                        h_bank[b, j][:, 2 * u + e, :],
+                        normed[b, j][:, e, u * P : (u + 1) * P],
+                        ident[:],
                     )
-            h_t[i] = per_tile.tile([P, PACK, P], BF16, name="h_t")
+            if j == 0:
+                h_t[b] = per_batch.tile([P, PACK, J * P], BF16, name="h_t")
 
-        def gain_and_bias(i, t):
+        def gain_tile(b, j):
+            for t in range(PACK):
+                nc.scalar.activation(
+                    out=h_t[b][:, t, j * P : (j + 1) * P],
+                    in_=h_bank[b, j][:, t, :],
+                    func=ACT.Identity,
+                    bias=ln_cols[:, PACK + t : PACK + t + 1],
+                    scale=ln_cols[:, t : t + 1],
+                )
+
+        def regroup_tile(b, j):
+            if j == 0:
+                grouped_h[b] = per_batch.tile(
+                    [P, J * P, PACK], BF16, align_bytes=64, name="grouped_h"
+                )
+            tokens = slice(j * P, (j + 1) * P)
+            nc.vector.tensor_copy(
+                out=grouped_h[b][:, tokens, :].rearrange("q (c r) t -> q c t r", r=4),
+                in_=h_t[b][:, :, tokens].rearrange("q t (c r) -> q c t r", r=4),
+            )
+
+        def quantise_tile(b, j):
+            if j == 0:
+                h_codes[b] = per_batch.tile([P, J * P], U32, align_bytes=64, name="h_codes")
+                h_scales[b] = per_batch.tile([P, J * P], U8, align_bytes=64, name="h_scales")
+            tokens = slice(j * P, (j + 1) * P)
+            nc.vector.quantize_mx(
+                out=h_codes[b][:, tokens].bitcast(FP8X4),
+                scales=h_scales[b][:, tokens],
+                in_=grouped_h[b][:, tokens, :].rearrange("q s t -> q (s t)"),
+            )
+
+        def gain_and_bias(b, t):
+            u, e = divmod(t, 2)
             nc.scalar.activation(
-                out=h_t[i][:, t, :],
-                in_=h_bank[i][:, t, :],
+                out=h_t[b][:, t, :],
+                in_=h_bank[b, u][:, e, :, :].rearrange("q j s -> q (j s)"),
                 func=ACT.Identity,
                 bias=ln_cols[:, PACK + t : PACK + t + 1],
                 scale=ln_cols[:, t : t + 1],
             )
 
-        def gain_and_bias_calls(i):
-            return [lambda t=t: gain_and_bias(i, t) for t in range(PACK)]
-
-        def regroup_h(i):
-            grouped_h[i] = per_tile.tile([P, P, PACK], BF16, align_bytes=64, name="grouped_h")
+        def regroup_h(b):
+            grouped_h[b] = per_batch.tile([P, J * P, PACK], BF16, align_bytes=64, name="grouped_h")
             nc.vector.tensor_copy(
-                out=grouped_h[i][:].rearrange("q (c r) t -> q c t r", r=4),
-                in_=h_t[i][:].rearrange("q t (c r) -> q c t r", r=4),
+                out=grouped_h[b][:].rearrange("q (c r) t -> q c t r", r=4),
+                in_=h_t[b][:].rearrange("q t (c r) -> q c t r", r=4),
             )
 
-        def quantise_h(i):
-            h_codes[i] = per_tile.tile([P, P], U32, align_bytes=64, name="h_codes")
-            h_scales[i] = per_tile.tile([P, P], U8, align_bytes=64, name="h_scales")
+        def quantise_h(b):
+            h_codes[b] = per_batch.tile([P, J * P], U32, align_bytes=64, name="h_codes")
+            h_scales[b] = per_batch.tile([P, J * P], U8, align_bytes=64, name="h_scales")
             nc.vector.quantize_mx(
-                out=h_codes[i][:].bitcast(FP8X4),
-                scales=h_scales[i][:],
-                in_=grouped_h[i][:].rearrange("q s t -> q (s t)"),
+                out=h_codes[b][:].bitcast(FP8X4),
+                scales=h_scales[b][:],
+                in_=grouped_h[b][:].rearrange("q s t -> q (s t)"),
             )
 
         acc2 = {}
         heads = {}
 
-        def second_product(i, c):
+        def second_product(b, c, tiles=range(J)):
             cols = slice(c * D, (c + 1) * D)
-            acc2[i, c] = new_bank([P, D], "acc2")
-            nc.tensor.matmul_mx(
-                out=acc2[i, c][:],
-                lhsT=h_codes[i][:].bitcast(FP8X4),
-                lhsT_scale=h_scales[i][:],
-                rhs=wqkv_codes[:, cols].bitcast(FP8X4),
-                rhs_scale=wqkv_scales[:, cols],
-                start=True,
-                stop=True,
-            )
+            for j in tiles:
+                acc2[b, j, c] = new_bank([P, D], "acc2")
+                nc.tensor.matmul_mx(
+                    out=acc2[b, j, c][:],
+                    lhsT=h_codes[b][:, j * P : (j + 1) * P].bitcast(FP8X4),
+                    lhsT_scale=h_scales[b][:, j * P : (j + 1) * P],
+                    rhs=wqkv_codes[:, cols].bitcast(FP8X4),
+                    rhs_scale=wqkv_scales[:, cols],
+                    start=True,
+                    stop=True,
+                )
 
-        def add_bias(i, c):
-            b, j = divmod(i, J)
+        def add_bias(b, j, c):
             cols = slice(c * D, (c + 1) * D)
             if j == 0:
                 heads[b, c] = results.tile([P, NH, J, HD], F32, name="heads")
             nc.vector.tensor_tensor(
                 out=heads[b, c][:, :, j, :],
-                in0=acc2[i, c][:].rearrange("p (n d) -> p n d", n=NH),
-                in1=bq_bc[:, cols].rearrange("p (n d) -> p n d", n=NH),
+                in0=acc2[b, j, c][:].rearrange("p (n d) -> p n d", n=NH),
+                in1=bias_bc[:, cols].rearrange("p (n d) -> p n d", n=NH),
                 op=ALU.add,
             )
             if j == J - 1:
@@ -309,120 +420,193 @@ def tile_block_pa_kernel(
                     in_=heads[b, c][:].rearrange("p n j d -> p n (j d)"),
                 )
 
-        def nothing():
-            return None
-
-        bo_bc = keep.tile([P, D], BF16)
-        bq_bc = keep.tile([P, N_QKV * D], BF16)
+        bias_bc = keep.tile([P, (N_QKV + 1) * D], BF16)
         wo_codes = keep.tile([P, D], U32, align_bytes=64)
         wo_scales = keep.tile([P, D], U8, align_bytes=64)
         wqkv_codes = keep.tile([P, N_QKV * D], U32, align_bytes=64)
         wqkv_scales = keep.tile([P, N_QKV * D], U8, align_bytes=64)
-        qkv_cols = [slice(c * D, (c + 1) * D) for c in range(N_QKV)]
+        ln_pairs = keep.tile([P, 2 * PACK], BF16)
+        ln_cols = keep.tile([P, 2 * PACK], F32)
+        on_scalar = nc.scalar.copy
+        on_vector = nc.vector.tensor_copy
 
+        def quantise_wo_half(half):
+            cols = slice(half * 2 * P, (half + 1) * 2 * P)
+            nc.vector.quantize_mx(
+                out=wo_codes[:, cols].bitcast(FP8X4),
+                scales=wo_scales[:, cols],
+                in_=grouped_w["o"][:, half * 2 * D : (half + 1) * 2 * D],
+            )
+
+        def quantise_qkv_weight(c):
+            cols = slice(c * D, (c + 1) * D)
+            quantise_weight(c, wqkv_codes[:, cols], wqkv_scales[:, cols])
+
+        bias_bank = {}
+
+        def spread_bias(first, width):
+            bias_bank[first] = new_bank([P, width * D], "bias_bank", BF16)
+            for part in range(width):
+                cols = slice((first + part) * D, (first + part + 1) * D)
+                nc.tensor.matmul(
+                    out=bias_bank[first][:, part * D : (part + 1) * D],
+                    lhsT=ones[:],
+                    rhs=bias_rows[:, cols],
+                    start=True,
+                    stop=True,
+                )
+
+        def copy_bias(first, width):
+            nc.vector.tensor_copy(
+                out=bias_bc[:, first * D : (first + width) * D], in_=bias_bank[first][:]
+            )
+
+        spread_bias(N_QKV, 1)
+        copy_bias(N_QKV, 1)
         turn_o(0)
         copy_o(0)
         quantise_o(0)
-        bo_bank = spread_bias(bo_rows[:])
-        nc.vector.tensor_copy(out=bo_bc[:], in_=bo_bank[:])
-
+        turn_weight("o", wo_sb)
         ln_bank = new_bank([P, P], "ln_bank")
         nc.tensor.transpose(ln_bank[:], ln_rows[:].bitcast(F32), ident[:])
-        ln_pairs = keep.tile([P, 2 * PACK], BF16)
+        spread_bias(0, 2)
+        spread_bias(2, 1)
+        copy_weight(on_scalar, "o", 0)
+        copy_weight(on_scalar, "o", 1)
+        add_bias_to_x(nc.vector, 0, 0)
+        add_bias_to_x(nc.vector, 0, 1)
+        quantise_wo_half(0)
+        quantise_wo_half(1)
         nc.vector.tensor_copy(out=ln_pairs[:].bitcast(F32), in_=ln_bank[:, 0:PACK])
-        ln_cols = keep.tile([P, 2 * PACK], F32)
+        copy_bias(0, 2)
+        copy_bias(2, 1)
         nc.vector.tensor_copy(out=ln_cols[:], in_=ln_pairs[:])
-
-        wo_halves = turn_weight(wo_sb)
-        grouped_wo = new_grouped_weight()
-        copy_weight_half(nc.scalar.copy, wo_halves, grouped_wo, 0)
-        copy_weight_half(nc.vector.tensor_copy, wo_halves, grouped_wo, 1)
-        quantise_weight(grouped_wo, wo_codes[:], wo_scales[:])
-
-        bq_banks = [spread_bias(bq_rows[:, cols]) for cols in qkv_cols]
-        nc.scalar.copy(out=bq_bc[:, qkv_cols[0]], in_=bq_banks[0][:])
-        nc.scalar.copy(out=bq_bc[:, qkv_cols[1]], in_=bq_banks[1][:])
-        nc.vector.tensor_copy(out=bq_bc[:, qkv_cols[2]], in_=bq_banks[2][:])
-
+        first_product(0)
+        add_residual(0, 0)
+        add_residual(0, 1)
+        turn_weight(0, wqkv_sb[0])
         turn_o(1)
+        copy_weight(on_vector, 0, 0)
+        copy_weight(on_vector, 0, 1)
+        mean(0, 0)
+        deviations(0, 0)
+        mean(0, 1)
+        inverse_deviation(0, 0, 1)
+        deviations(0, 1)
         copy_o(1)
+        inverse_deviation(0, 1, 1)
+        normalise_on_vector(0, 0)
+        quantise_qkv_weight(0)
+        normalise_on_vector(0, 1)
+        turn_h_tile(0, 0)
+        turn_weight(1, wqkv_sb[1])
+        turn_h_tile(0, 1)
+        gain_tile(0, 0)
+        copy_weight(on_scalar, 1, 0)
+        gain_tile(0, 1)
         quantise_o(1)
-        for i in range(TILES):
-            add_bias_to_x(i)
-        for i in range(2 * J):
-            first_product(i)
-        for i in range(2 * J):
-            add_residual(i)
-
-        w_halves = [turn_weight(wqkv_sb[c]) for c in range(N_QKV)]
-        grouped_w = [new_grouped_weight() for c in range(N_QKV)]
+        add_bias_to_x(nc.vector, 1, 0)
+        add_bias_to_x(nc.vector, 1, 1)
+        first_product(1)
+        turn_weight(2, wqkv_sb[2])
+        regroup_tile(0, 0)
+        add_residual(1, 0)
+        quantise_tile(0, 0)
+        add_residual(1, 1)
+        copy_weight(on_scalar, 1, 1)
+        mean(1, 0)
+        deviations(1, 0)
+        regroup_tile(0, 1)
+        quantise_qkv_weight(1)
+        quantise_tile(0, 1)
+        second_product(0, 0)
+        second_product(0, 1)
+        copy_weight(on_scalar, 2, 0)
+        mean(1, 1)
+        deviations(1, 1)
+        copy_weight(on_scalar, 2, 1)
+        inverse_deviation(1)
         turn_o(2)
-        layer_norm(0, [nothing] * PACK)
-        turn_h(0)
-        for c in range(2):
-            for half in range(2):
-                copy_weight_half(nc.vector.tensor_copy, w_halves[c], grouped_w[c], half)
-        for c in range(2):
-            quantise_weight(grouped_w[c], wqkv_codes[:, qkv_cols[c]], wqkv_scales[:, qkv_cols[c]])
-        turn_o(3)
-        layer_norm(1, gain_and_bias_calls(0))
-        turn_h(1)
+        for j in range(J):
+            sum_bias_and_x(2, j)
         copy_o(2)
-        for half in range(2):
-            copy_weight_half(nc.vector.tensor_copy, w_halves[2], grouped_w[2], half)
-        regroup_h(0)
-        quantise_weight(grouped_w[2], wqkv_codes[:, qkv_cols[2]], wqkv_scales[:, qkv_cols[2]])
-        quantise_h(0)
+        shift_tile(1, 0)
+        normalise(1, 0)
+        copy_bias_and_x(2, 0)
+        add_bias(0, 0, 0)
+        add_bias(0, 1, 0)
+        normalise_on_vector(1, 1)
+        add_bias(0, 0, 1)
         quantise_o(2)
-        for i in range(2 * J, 3 * J):
-            first_product(i)
-        for i in range(2 * J, 3 * J):
-            add_residual(i)
-        layer_norm(2, gain_and_bias_calls(1))
-        turn_h(2)
-        copy_o(3)
+        quantise_qkv_weight(2)
+        add_bias(0, 1, 1)
+        turn_h(1)
+        first_product(2)
+        second_product(0, 2)
+        for t in range(PACK):
+            gain_and_bias(1, t)
+        copy_bias_and_x(2, 1)
+        add_residual(2, 0)
+        add_bias(0, 0, 2)
+        add_residual(2, 1)
+        add_bias(0, 1, 2)
         regroup_h(1)
+        mean(2, 0)
+        mean(2, 1)
+        turn_o(3)
+        for j in range(J):
+            sum_bias_and_x(3, j)
+        deviations(2, 0)
+        copy_o(3)
+        deviations(2, 1)
         quantise_o(3)
         quantise_h(1)
-        for i in range(3 * J, 4 * J):
-            first_product(i)
-        for i in range(3 * J, 4 * J):
-            add_residual(i)
-
-        def scalar_step(i):
-            if i < TILES:
-                layer_norm(i, gain_and_bias_calls(i - 1))
-                turn_h(i)
-            elif i - 1 < TILES:
-                for call in gain_and_bias_calls(i - 1):
-                    call()
-
-        for b in range(B):
-            i0 = J * b
-            i1 = i0 + 1
-            more = b + 1 < B
-
-            second_product(i0, 0)
-            second_product(i1, 0)
-            scalar_step(i0 + 3)
-            add_bias(i0, 0)
-            add_bias(i1, 0)
-            if more:
-                regroup_h(i0 + 2)
-
-            second_product(i0, 1)
-            second_product(i1, 1)
-            add_bias(i0, 1)
-            if more:
-                quantise_h(i0 + 2)
-            add_bias(i1, 1)
-            scalar_step(i0 + 4)
-            if more:
-                regroup_h(i0 + 3)
-
-            second_product(i0, 2)
-            second_product(i1, 2)
-            add_bias(i0, 2)
-            if more:
-                quantise_h(i0 + 3)
-            add_bias(i1, 2)
+        first_product(3)
+        second_product(1, 0)
+        inverse_deviation(2)
+        copy_bias_and_x(3, 0)
+        shift_tile(2, 0)
+        copy_bias_and_x(3, 1)
+        normalise(2, 0)
+        add_bias(1, 0, 0)
+        add_bias(1, 1, 0)
+        normalise_on_vector(2, 1)
+        second_product(1, 1)
+        turn_h(2)
+        add_residual(3, 0)
+        add_residual(3, 1)
+        for t in range(PACK):
+            gain_and_bias(2, t)
+        second_product(1, 2)
+        add_bias(1, 0, 1)
+        add_bias(1, 1, 1)
+        mean(3, 0)
+        mean(3, 1)
+        deviations(3, 0)
+        deviations(3, 1)
+        inverse_deviation(3)
+        shift_tile(3, 0)
+        normalise(3, 0)
+        regroup_h(2)
+        add_bias(1, 0, 2)
+        quantise_h(2)
+        normalise_on_vector(3, 1)
+        add_bias(1, 1, 2)
+        second_product(2, 0)
+        turn_h(3)
+        second_product(2, 1)
+        for t in range(PACK):
+            gain_and_bias(3, t)
+        add_bias(2, 0, 0)
+        add_bias(2, 1, 0)
+        add_bias(2, 0, 1)
+        regroup_h(3)
+        add_bias(2, 1, 1)
+        quantise_h(3)
+        second_product(2, 2)
+        add_bias(2, 0, 2)
+        add_bias(2, 1, 2)
+        for c in range(N_QKV):
+            second_product(3, c)
+            for j in range(J):
+                add_bias(3, j, c)

@@ -40,6 +40,7 @@ def tile_block_pa_kernel(
         per_weight = stack.enter_context(tc.tile_pool(name="per_weight", bufs=1 + N_QKV))
         per_batch = stack.enter_context(tc.tile_pool(name="per_batch", bufs=B))
         per_tile = stack.enter_context(tc.tile_pool(name="per_tile", bufs=B * J))
+        shared = stack.enter_context(tc.tile_pool(name="shared", bufs=1))
         results = stack.enter_context(tc.tile_pool(name="results", bufs=2 * N_QKV))
         banks = stack.enter_context(tc.psum_pool(name="banks", bufs=PSUM_BANKS))
         stack.enter_context(tc.manual_schedule())
@@ -85,22 +86,23 @@ def tile_block_pa_kernel(
 
         bo_cols = slice(N_QKV * D, (N_QKV + 1) * D)
         make_identity(nc, ident[:])
-        nc.scalar.dma_start(
-            out=bias_rows[0:1, bo_cols], in_=bo_l.rearrange("(o d) -> o d", o=1)
-        )
-        nc.gpsimd.dma_start(out=ln_rows[0:2, :], in_=ln2_w.rearrange("(u c) -> u c", u=2))
-        nc.gpsimd.dma_start(out=ln_rows[2:4, :], in_=ln2_b.rearrange("(u c) -> u c", u=2))
-        nc.gpsimd.dma_start(
-            out=bias_rows[0:1, 0 : N_QKV * D], in_=bqkv_g.rearrange("(o d) -> o d", o=1)
-        )
+        def load_row(tile, row, cols, vector, rows=1):
+            nc.sync.dma_start(
+                out=tile[row : row + rows, cols], in_=vector.rearrange("(u c) -> u c", u=rows)
+            )
+
         load_o(0)
+        load_row(bias_rows, 0, bo_cols, bo_l)
         for half in range(2):
             load_weight_half(wo_sb, Wo_l, half)
         load_x(0)
         load_weight(wqkv_sb[0], Wqkv_g[0:D, :])
         load_o(1)
         load_x(1)
+        load_row(ln_rows, 0, slice(0, 2 * P), ln2_w, 2)
+        load_row(ln_rows, 2, slice(0, 2 * P), ln2_b, 2)
         load_weight(wqkv_sb[1], Wqkv_g[D : 2 * D, :])
+        load_row(bias_rows, 0, slice(0, N_QKV * D), bqkv_g)
         load_weight(wqkv_sb[2], Wqkv_g[2 * D : 3 * D, :])
         for b in range(2, B):
             load_o(b)
@@ -122,7 +124,14 @@ def tile_block_pa_kernel(
 
         def turn_weight(c, w_sb):
             words = w_sb[:].bitcast(F32)
-            grouped_w[c] = per_weight.tile([P, PACK * D], BF16, align_bytes=64, name="grouped_w")
+            if c == 2:
+                grouped_w[c] = shared.tile(
+                    [P, PACK * D], BF16, align_bytes=64, name="grouped_w2", tag="late"
+                )
+            else:
+                grouped_w[c] = per_weight.tile(
+                    [P, PACK * D], BF16, align_bytes=64, name="grouped_w"
+                )
             for half in range(2):
                 w_bank[c, half] = new_bank([P, 2, 2, P], "w_bank")
                 for tt in range(2):
@@ -169,14 +178,23 @@ def tile_block_pa_kernel(
                 out=o_codes[b][:].bitcast(FP8X4), scales=o_scales[b][:], in_=grouped_o[b][:]
             )
 
-        xb = [per_batch.tile([P, J, D], F32, name="xb") for b in range(B)]
+        xb = {}
+        xb3 = []
         x_loc = [per_batch.tile([P, J, D], F32, name="x_loc") for b in range(B)]
         sums = [per_batch.tile([P, J], F32, name="sums") for b in range(B)]
         acc1 = {}
 
         def add_bias_to_x(engine, b, j):
+            if b == 2 and j == 0:
+                xb[b, j] = shared.tile([P, D], F32, name="xb2", tag="early", align_bytes=64)
+            elif b == 3:
+                if j == 0:
+                    xb3.append(shared.tile([P, J, D], F32, name="xb3", tag="late", align_bytes=64))
+                xb[b, j] = xb3[0][:, j, :]
+            else:
+                xb[b, j] = per_tile.tile([P, D], F32, name="xb")
             engine.tensor_tensor(
-                out=xb[b][:, j, :],
+                out=xb[b, j] if b == 3 else xb[b, j][:],
                 in0=x_sb[b][:, j * D : (j + 1) * D],
                 in1=bias_bc[:, bo_cols],
                 op=ALU.add,
@@ -198,7 +216,8 @@ def tile_block_pa_kernel(
             )
 
         def copy_bias_and_x(b, j):
-            nc.scalar.copy(out=xb[b][:, j, :], in_=x_bank[b, j][:])
+            xb[b, j] = per_tile.tile([P, D], F32, name="xb")
+            nc.scalar.copy(out=xb[b, j][:], in_=x_bank[b, j][:])
 
         def first_product(b):
             for j in range(J):
@@ -218,7 +237,7 @@ def tile_block_pa_kernel(
                 out=x_loc[b][:, j, :],
                 in0=acc1[b, j][:],
                 scalar=1.0,
-                in1=xb[b][:, j, :],
+                in1=xb[b, j] if b == 3 else xb[b, j][:],
                 op0=ALU.mult,
                 op1=ALU.add,
                 accum_out=sums[b][:, j : j + 1],
@@ -240,13 +259,21 @@ def tile_block_pa_kernel(
         h_codes = [None] * B
         h_scales = [None] * B
 
-        def mean(b, j):
-            if j == 0:
-                neg_mean[b] = per_batch.tile([P, J], F32, name="neg_mean")
-                sum_sq[b] = per_batch.tile([P, J], F32, name="sum_sq")
-                shift[b] = per_batch.tile([P, J], F32, name="shift")
-            nc.scalar.mul(
-                out=neg_mean[b][:, j : j + 1], in_=sums[b][:, j : j + 1], mul=-1.0 / D
+        def new_statistics(b):
+            neg_mean[b] = per_batch.tile([P, J], F32, name="neg_mean")
+            sum_sq[b] = per_batch.tile([P, J], F32, name="sum_sq")
+            shift[b] = per_batch.tile([P, J], F32, name="shift")
+
+        def mean(b, first=0, count=J):
+            if first == 0:
+                new_statistics(b)
+            nc.gpsimd.tensor_scalar(
+                out=neg_mean[b][:, first : first + count],
+                in0=sums[b][:, first : first + count],
+                scalar1=-1.0 / D,
+                scalar2=0.0,
+                op0=ALU.mult,
+                op1=ALU.add,
             )
 
         def deviations(b, j):
@@ -341,8 +368,8 @@ def tile_block_pa_kernel(
 
         def regroup_tile(b, j):
             if j == 0:
-                grouped_h[b] = per_batch.tile(
-                    [P, J * P, PACK], BF16, align_bytes=64, name="grouped_h"
+                grouped_h[b] = shared.tile(
+                    [P, J * P, PACK], BF16, align_bytes=64, name="grouped_h0", tag="early"
                 )
             tokens = slice(j * P, (j + 1) * P)
             nc.vector.tensor_copy(
@@ -404,9 +431,54 @@ def tile_block_pa_kernel(
                     stop=True,
                 )
 
+        def add_bias_late(b, j, c):
+            cols = slice(c * D, (c + 1) * D)
+            if (b, c) not in heads:
+                heads[b, c] = results.tile([P, NH, J, HD], F32, name="heads")
+            product = per_tile.tile([P, D], F32, name="product")
+            nc.scalar.copy(out=product[:], in_=acc2[b, j, c][:])
+            nc.gpsimd.tensor_tensor(
+                out=heads[b, c][:, :, j, :],
+                in0=product[:].rearrange("p (n d) -> p n d", n=NH),
+                in1=bias_bc[:, cols].rearrange("p (n d) -> p n d", n=NH),
+                op=ALU.add,
+            )
+            store_when_complete(b, c)
+
+        done = []
+
+        def store_when_complete(b, c):
+            done.append((b, c))
+            if done.count((b, c)) == J:
+                store_heads(b, c)
+
+        def store_heads(b, c):
+            nc.sync.dma_start(
+                out=qkv_out[c][b].rearrange("n (p j) d -> p n (j d)", j=J),
+                in_=heads[b, c][:].rearrange("p n j d -> p n (j d)"),
+            )
+
+        def add_bias_heads(b, j, c, first, count):
+            cols = slice(c * D + first * HD, c * D + (first + count) * HD)
+            if (b, c) not in heads:
+                heads[b, c] = results.tile([P, NH, J, HD], F32, name="heads")
+            nc.vector.tensor_tensor(
+                out=heads[b, c][:, first : first + count, j, :],
+                in0=acc2[b, j, c][:, first * HD : (first + count) * HD].rearrange(
+                    "p (n d) -> p n d", n=count
+                ),
+                in1=bias_bc[:, cols].rearrange("p (n d) -> p n d", n=count),
+                op=ALU.add,
+            )
+            if j == J - 1:
+                nc.sync.dma_start(
+                    out=qkv_out[c][b, first : first + count].rearrange("n (p j) d -> p n (j d)", j=J),
+                    in_=heads[b, c][:, first : first + count].rearrange("p n j d -> p n (j d)"),
+                )
+
         def add_bias(b, j, c):
             cols = slice(c * D, (c + 1) * D)
-            if j == 0:
+            if (b, c) not in heads:
                 heads[b, c] = results.tile([P, NH, J, HD], F32, name="heads")
             nc.vector.tensor_tensor(
                 out=heads[b, c][:, :, j, :],
@@ -414,11 +486,7 @@ def tile_block_pa_kernel(
                 in1=bias_bc[:, cols].rearrange("p (n d) -> p n d", n=NH),
                 op=ALU.add,
             )
-            if j == J - 1:
-                nc.sync.dma_start(
-                    out=qkv_out[c][b].rearrange("n (p j) d -> p n (j d)", j=J),
-                    in_=heads[b, c][:].rearrange("p n j d -> p n (j d)"),
-                )
+            store_when_complete(b, c)
 
         bias_bc = keep.tile([P, (N_QKV + 1) * D], BF16)
         wo_codes = keep.tile([P, D], U32, align_bytes=64)
@@ -456,157 +524,152 @@ def tile_block_pa_kernel(
                     stop=True,
                 )
 
-        def copy_bias(first, width):
-            nc.vector.tensor_copy(
+        def copy_bias(copy, first, width):
+            copy(
                 out=bias_bc[:, first * D : (first + width) * D], in_=bias_bank[first][:]
             )
 
-        spread_bias(N_QKV, 1)
-        copy_bias(N_QKV, 1)
         turn_o(0)
         copy_o(0)
+        spread_bias(N_QKV, 1)
+        copy_bias(on_vector, N_QKV, 1)
         quantise_o(0)
         turn_weight("o", wo_sb)
-        ln_bank = new_bank([P, P], "ln_bank")
-        nc.tensor.transpose(ln_bank[:], ln_rows[:].bitcast(F32), ident[:])
-        spread_bias(0, 2)
-        spread_bias(2, 1)
         copy_weight(on_scalar, "o", 0)
         copy_weight(on_scalar, "o", 1)
         add_bias_to_x(nc.vector, 0, 0)
-        add_bias_to_x(nc.vector, 0, 1)
         quantise_wo_half(0)
         quantise_wo_half(1)
-        nc.vector.tensor_copy(out=ln_pairs[:].bitcast(F32), in_=ln_bank[:, 0:PACK])
-        copy_bias(0, 2)
-        copy_bias(2, 1)
-        nc.vector.tensor_copy(out=ln_cols[:], in_=ln_pairs[:])
+        add_bias_to_x(nc.vector, 0, 1)
         first_product(0)
-        add_residual(0, 0)
-        add_residual(0, 1)
         turn_weight(0, wqkv_sb[0])
         turn_o(1)
-        copy_weight(on_vector, 0, 0)
-        copy_weight(on_vector, 0, 1)
-        mean(0, 0)
+        add_residual(0, 0)
+        add_residual(0, 1)
+        mean(0, 0, 1)
+        mean(0, 1, 1)
+        add_bias_to_x(nc.gpsimd, 1, 0)
         deviations(0, 0)
-        mean(0, 1)
-        inverse_deviation(0, 0, 1)
         deviations(0, 1)
+        inverse_deviation(0, 0, 1)
         copy_o(1)
         inverse_deviation(0, 1, 1)
+        copy_weight(on_vector, 0, 0)
+        copy_weight(on_vector, 0, 1)
         normalise_on_vector(0, 0)
-        quantise_qkv_weight(0)
-        normalise_on_vector(0, 1)
-        turn_h_tile(0, 0)
-        turn_weight(1, wqkv_sb[1])
-        turn_h_tile(0, 1)
-        gain_tile(0, 0)
-        copy_weight(on_scalar, 1, 0)
-        gain_tile(0, 1)
         quantise_o(1)
-        add_bias_to_x(nc.vector, 1, 0)
-        add_bias_to_x(nc.vector, 1, 1)
+        normalise_on_vector(0, 1)
+        quantise_qkv_weight(0)
+        ln_bank = new_bank([P, P], "ln_bank")
+        nc.tensor.transpose(ln_bank[:], ln_rows[:].bitcast(F32), ident[:])
+        turn_h_tile(0, 0)
+        nc.scalar.copy(out=ln_pairs[:].bitcast(F32), in_=ln_bank[:, 0:PACK])
+        nc.scalar.copy(out=ln_cols[:], in_=ln_pairs[:])
+        gain_tile(0, 0)
         first_product(1)
-        turn_weight(2, wqkv_sb[2])
-        regroup_tile(0, 0)
+        turn_h_tile(0, 1)
+        gain_tile(0, 1)
+        turn_weight(1, wqkv_sb[1])
+        copy_weight(on_scalar, 1, 0)
+        copy_weight(on_scalar, 1, 1)
+        spread_bias(0, 2)
+        copy_bias(on_scalar, 0, 2)
+        turn_o(2)
         add_residual(1, 0)
+        regroup_tile(0, 0)
+        add_bias_to_x(nc.vector, 1, 1)
         quantise_tile(0, 0)
         add_residual(1, 1)
-        copy_weight(on_scalar, 1, 1)
-        mean(1, 0)
-        deviations(1, 0)
+        mean(1)
         regroup_tile(0, 1)
         quantise_qkv_weight(1)
         quantise_tile(0, 1)
+        for j in range(J):
+            add_bias_to_x(nc.gpsimd, 2, j)
         second_product(0, 0)
         second_product(0, 1)
-        copy_weight(on_scalar, 2, 0)
-        mean(1, 1)
+        deviations(1, 0)
         deviations(1, 1)
-        copy_weight(on_scalar, 2, 1)
-        inverse_deviation(1)
-        turn_o(2)
-        for j in range(J):
-            sum_bias_and_x(2, j)
         copy_o(2)
-        shift_tile(1, 0)
-        normalise(1, 0)
-        copy_bias_and_x(2, 0)
-        add_bias(0, 0, 0)
-        add_bias(0, 1, 0)
-        normalise_on_vector(1, 1)
-        add_bias(0, 0, 1)
+        inverse_deviation(1)
+        turn_weight(2, wqkv_sb[2])
+        spread_bias(2, 1)
+        copy_weight(on_scalar, 2, 0)
+        copy_weight(on_scalar, 2, 1)
+        copy_bias(on_scalar, 2, 1)
+        for c in range(2):
+            for j in range(J):
+                add_bias(0, j, c)
         quantise_o(2)
+        normalise_on_vector(1, 0)
+        normalise_on_vector(1, 1)
         quantise_qkv_weight(2)
-        add_bias(0, 1, 1)
-        turn_h(1)
+        for j in range(J):
+            add_bias_to_x(nc.gpsimd, 3, j)
         first_product(2)
+        turn_h(1)
         second_product(0, 2)
         for t in range(PACK):
             gain_and_bias(1, t)
-        copy_bias_and_x(2, 1)
         add_residual(2, 0)
-        add_bias(0, 0, 2)
         add_residual(2, 1)
+        mean(2)
+        turn_o(3)
+        copy_o(3)
+        deviations(2, 0)
+        deviations(2, 1)
+        inverse_deviation(2)
+        add_bias(0, 0, 2)
         add_bias(0, 1, 2)
         regroup_h(1)
-        mean(2, 0)
-        mean(2, 1)
-        turn_o(3)
-        for j in range(J):
-            sum_bias_and_x(3, j)
-        deviations(2, 0)
-        copy_o(3)
-        deviations(2, 1)
         quantise_o(3)
         quantise_h(1)
         first_product(3)
         second_product(1, 0)
-        inverse_deviation(2)
-        copy_bias_and_x(3, 0)
-        shift_tile(2, 0)
-        copy_bias_and_x(3, 1)
-        normalise(2, 0)
-        add_bias(1, 0, 0)
-        add_bias(1, 1, 0)
+        normalise_on_vector(2, 0)
         normalise_on_vector(2, 1)
-        second_product(1, 1)
+        add_bias(1, 0, 0)
         turn_h(2)
+        second_product(1, 1)
         add_residual(3, 0)
+        add_bias(1, 1, 0)
         add_residual(3, 1)
+        mean(3)
         for t in range(PACK):
             gain_and_bias(2, t)
         second_product(1, 2)
-        add_bias(1, 0, 1)
-        add_bias(1, 1, 1)
-        mean(3, 0)
-        mean(3, 1)
         deviations(3, 0)
+        add_bias_late(1, 1, 1)
         deviations(3, 1)
         inverse_deviation(3)
-        shift_tile(3, 0)
-        normalise(3, 0)
+        add_bias(1, 0, 1)
         regroup_h(2)
         add_bias(1, 0, 2)
         quantise_h(2)
-        normalise_on_vector(3, 1)
-        add_bias(1, 1, 2)
         second_product(2, 0)
+        add_bias(1, 1, 2)
+        normalise_on_vector(3, 0)
+        normalise_on_vector(3, 1)
         turn_h(3)
         second_product(2, 1)
+        add_bias(2, 0, 0)
         for t in range(PACK):
             gain_and_bias(3, t)
-        add_bias(2, 0, 0)
         add_bias(2, 1, 0)
+        second_product(2, 2)
+        add_bias_late(2, 1, 1)
         add_bias(2, 0, 1)
         regroup_h(3)
-        add_bias(2, 1, 1)
-        quantise_h(3)
-        second_product(2, 2)
         add_bias(2, 0, 2)
+        quantise_h(3)
+        second_product(3, 0)
+        second_product(3, 1)
+        second_product(3, 2)
         add_bias(2, 1, 2)
-        for c in range(N_QKV):
-            second_product(3, c)
+        add_bias_late(3, 0, 0)
+        add_bias(3, 1, 0)
+        add_bias(3, 0, 1)
+        add_bias(3, 1, 1)
+        for first in (0, 2):
             for j in range(J):
-                add_bias(3, j, c)
+                add_bias_heads(3, j, 2, first, 2)

@@ -42,7 +42,8 @@ def tile_block_pa_kernel(
         per_tile = stack.enter_context(tc.tile_pool(name="per_tile", bufs=B * J))
         shared = stack.enter_context(tc.tile_pool(name="shared", bufs=1))
         results = stack.enter_context(tc.tile_pool(name="results", bufs=2 * N_QKV))
-        banks = stack.enter_context(tc.psum_pool(name="banks", bufs=PSUM_BANKS))
+        banks = stack.enter_context(tc.psum_pool(name="banks", bufs=PSUM_BANKS - 1))
+        spare = stack.enter_context(tc.psum_pool(name="spare", bufs=1))
         stack.enter_context(tc.manual_schedule())
 
         bias_rows = keep.tile([P, (N_QKV + 1) * D], BF16)
@@ -54,6 +55,8 @@ def tile_block_pa_kernel(
         nc.vector.memset(eps_col[:], EPS)
         ones = keep.tile([P, P], BF16)
         nc.vector.memset(ones[:], 1.0)
+        zeros = keep.tile([P, D], BF16)
+        nc.gpsimd.memset(zeros[:].bitcast(I32), 0)
         ident = keep.tile([P, P], F32)
         ident_bf = keep.tile([P, P], BF16)
 
@@ -118,6 +121,26 @@ def tile_block_pa_kernel(
 
         def turn_words(bank, words, first_word):
             nc.tensor.transpose(bank, words[:, first_word : first_word + P], ident[:])
+
+        spare_bank = spare.tile([P, D], F32)
+
+        def keep_busy_plain(count):
+            for i in range(count):
+                nc.tensor.matmul(
+                    out=spare_bank[:], lhsT=ones[:], rhs=zeros[:], start=True, stop=True
+                )
+
+        def keep_busy(count):
+            for i in range(count):
+                nc.tensor.matmul_mx(
+                    out=spare_bank[:],
+                    lhsT=o_codes[0][:, 0:P].bitcast(FP8X4),
+                    lhsT_scale=o_scales[0][:, 0:P],
+                    rhs=wo_codes[:].bitcast(FP8X4),
+                    rhs_scale=wo_scales[:],
+                    start=True,
+                    stop=True,
+                )
 
         w_bank = {}
         grouped_w = {}
@@ -529,12 +552,14 @@ def tile_block_pa_kernel(
                 out=bias_bc[:, first * D : (first + width) * D], in_=bias_bank[first][:]
             )
 
+        keep_busy_plain(4)
         turn_o(0)
         copy_o(0)
         spread_bias(N_QKV, 1)
         copy_bias(on_vector, N_QKV, 1)
         quantise_o(0)
         turn_weight("o", wo_sb)
+        keep_busy_plain(3)
         copy_weight(on_scalar, "o", 0)
         copy_weight(on_scalar, "o", 1)
         add_bias_to_x(nc.vector, 0, 0)
@@ -560,6 +585,7 @@ def tile_block_pa_kernel(
         quantise_o(1)
         normalise_on_vector(0, 1)
         quantise_qkv_weight(0)
+        keep_busy(4)
         ln_bank = new_bank([P, P], "ln_bank")
         nc.tensor.transpose(ln_bank[:], ln_rows[:].bitcast(F32), ident[:])
         turn_h_tile(0, 0)
@@ -586,7 +612,9 @@ def tile_block_pa_kernel(
         quantise_tile(0, 1)
         for j in range(J):
             add_bias_to_x(nc.gpsimd, 2, j)
-        second_product(0, 0)
+        second_product(0, 0, [0])
+        keep_busy(4)
+        second_product(0, 0, [1])
         second_product(0, 1)
         deviations(1, 0)
         deviations(1, 1)
@@ -594,6 +622,7 @@ def tile_block_pa_kernel(
         inverse_deviation(1)
         turn_weight(2, wqkv_sb[2])
         spread_bias(2, 1)
+        keep_busy(2)
         copy_weight(on_scalar, 2, 0)
         copy_weight(on_scalar, 2, 1)
         copy_bias(on_scalar, 2, 1)
@@ -615,6 +644,7 @@ def tile_block_pa_kernel(
         add_residual(2, 1)
         mean(2)
         turn_o(3)
+        keep_busy(6)
         copy_o(3)
         deviations(2, 0)
         deviations(2, 1)
@@ -646,6 +676,7 @@ def tile_block_pa_kernel(
         regroup_h(2)
         add_bias(1, 0, 2)
         quantise_h(2)
+        keep_busy(4)
         second_product(2, 0)
         add_bias(1, 1, 2)
         normalise_on_vector(3, 0)
@@ -662,6 +693,7 @@ def tile_block_pa_kernel(
         regroup_h(3)
         add_bias(2, 0, 2)
         quantise_h(3)
+        keep_busy(7)
         second_product(3, 0)
         second_product(3, 1)
         second_product(3, 2)

@@ -208,16 +208,9 @@ def tile_block_pa_kernel(
         acc1 = {}
 
         def add_bias_to_x(engine, b, j):
-            if b == 2 and j == 0:
-                xb[b, j] = shared.tile([P, D], F32, name="xb2", tag="early", align_bytes=64)
-            elif b == 3:
-                if j == 0:
-                    xb3.append(shared.tile([P, J, D], F32, name="xb3", tag="late", align_bytes=64))
-                xb[b, j] = xb3[0][:, j, :]
-            else:
-                xb[b, j] = per_tile.tile([P, D], F32, name="xb")
+            xb[b, j] = per_tile.tile([P, D], F32, name="xb")
             engine.tensor_tensor(
-                out=xb[b, j] if b == 3 else xb[b, j][:],
+                out=xb[b, j][:],
                 in0=x_sb[b][:, j * D : (j + 1) * D],
                 in1=bias_bc[:, bo_cols],
                 op=ALU.add,
@@ -260,7 +253,7 @@ def tile_block_pa_kernel(
                 out=x_loc[b][:, j, :],
                 in0=acc1[b, j][:],
                 scalar=1.0,
-                in1=xb[b, j] if b == 3 else xb[b, j][:],
+                in1=xb[b, j][:],
                 op0=ALU.mult,
                 op1=ALU.add,
                 accum_out=sums[b][:, j : j + 1],
@@ -290,13 +283,10 @@ def tile_block_pa_kernel(
         def mean(b, first=0, count=J):
             if first == 0:
                 new_statistics(b)
-            nc.gpsimd.tensor_scalar(
+            nc.scalar.mul(
                 out=neg_mean[b][:, first : first + count],
-                in0=sums[b][:, first : first + count],
-                scalar1=-1.0 / D,
-                scalar2=0.0,
-                op0=ALU.mult,
-                op1=ALU.add,
+                in_=sums[b][:, first : first + count],
+                mul=-1.0 / D,
             )
 
         def deviations(b, j):
@@ -552,14 +542,12 @@ def tile_block_pa_kernel(
                 out=bias_bc[:, first * D : (first + width) * D], in_=bias_bank[first][:]
             )
 
-        keep_busy_plain(4)
         turn_o(0)
         copy_o(0)
         spread_bias(N_QKV, 1)
         copy_bias(on_vector, N_QKV, 1)
         quantise_o(0)
         turn_weight("o", wo_sb)
-        keep_busy_plain(3)
         copy_weight(on_scalar, "o", 0)
         copy_weight(on_scalar, "o", 1)
         add_bias_to_x(nc.vector, 0, 0)
@@ -573,7 +561,6 @@ def tile_block_pa_kernel(
         add_residual(0, 1)
         mean(0, 0, 1)
         mean(0, 1, 1)
-        add_bias_to_x(nc.gpsimd, 1, 0)
         deviations(0, 0)
         deviations(0, 1)
         inverse_deviation(0, 0, 1)
@@ -585,6 +572,7 @@ def tile_block_pa_kernel(
         quantise_o(1)
         normalise_on_vector(0, 1)
         quantise_qkv_weight(0)
+        add_bias_to_x(nc.vector, 1, 0)
         keep_busy(4)
         ln_bank = new_bank([P, P], "ln_bank")
         nc.tensor.transpose(ln_bank[:], ln_rows[:].bitcast(F32), ident[:])
@@ -611,15 +599,16 @@ def tile_block_pa_kernel(
         quantise_qkv_weight(1)
         quantise_tile(0, 1)
         for j in range(J):
-            add_bias_to_x(nc.gpsimd, 2, j)
+            sum_bias_and_x(2, j)
         second_product(0, 0, [0])
-        keep_busy(4)
         second_product(0, 0, [1])
         second_product(0, 1)
         deviations(1, 0)
         deviations(1, 1)
         copy_o(2)
         inverse_deviation(1)
+        copy_bias_and_x(2, 0)
+        copy_bias_and_x(2, 1)
         turn_weight(2, wqkv_sb[2])
         spread_bias(2, 1)
         keep_busy(2)
@@ -633,8 +622,6 @@ def tile_block_pa_kernel(
         normalise_on_vector(1, 0)
         normalise_on_vector(1, 1)
         quantise_qkv_weight(2)
-        for j in range(J):
-            add_bias_to_x(nc.gpsimd, 3, j)
         first_product(2)
         turn_h(1)
         second_product(0, 2)
@@ -644,11 +631,14 @@ def tile_block_pa_kernel(
         add_residual(2, 1)
         mean(2)
         turn_o(3)
-        keep_busy(6)
+        for j in range(J):
+            sum_bias_and_x(3, j)
         copy_o(3)
         deviations(2, 0)
         deviations(2, 1)
         inverse_deviation(2)
+        copy_bias_and_x(3, 0)
+        copy_bias_and_x(3, 1)
         add_bias(0, 0, 2)
         add_bias(0, 1, 2)
         regroup_h(1)
@@ -669,7 +659,7 @@ def tile_block_pa_kernel(
             gain_and_bias(2, t)
         second_product(1, 2)
         deviations(3, 0)
-        add_bias_late(1, 1, 1)
+        add_bias(1, 1, 1)
         deviations(3, 1)
         inverse_deviation(3)
         add_bias(1, 0, 1)
@@ -688,7 +678,7 @@ def tile_block_pa_kernel(
             gain_and_bias(3, t)
         add_bias(2, 1, 0)
         second_product(2, 2)
-        add_bias_late(2, 1, 1)
+        add_bias(2, 1, 1)
         add_bias(2, 0, 1)
         regroup_h(3)
         add_bias(2, 0, 2)
@@ -698,7 +688,7 @@ def tile_block_pa_kernel(
         second_product(3, 1)
         second_product(3, 2)
         add_bias(2, 1, 2)
-        add_bias_late(3, 0, 0)
+        add_bias(3, 0, 0)
         add_bias(3, 1, 0)
         add_bias(3, 0, 1)
         add_bias(3, 1, 1)

@@ -77,14 +77,14 @@ def tile_block_pa_kernel(
 
         def load_weight(w_sb, rows):
             nc.sync.dma_start(
-                out=w_sb[:].rearrange("p (t k) -> p t k", k=D),
-                in_=rows.rearrange("(t p) k -> p t k", p=P),
+                out=w_sb[:].rearrange("p (h f) -> p h f", h=2),
+                in_=rows.rearrange("(h p t) k -> p h (t k)", h=2, p=P),
             )
 
         def load_weight_half(w_sb, rows, half):
             nc.sync.dma_start(
-                out=w_sb[:, half * 2 * D : (half + 1) * 2 * D].rearrange("p (t k) -> p t k", k=D),
-                in_=rows[half * 2 * P : (half + 1) * 2 * P, :].rearrange("(t p) k -> p t k", p=P),
+                out=w_sb[:, half * 2 * D : (half + 1) * 2 * D],
+                in_=rows[half * 2 * P : (half + 1) * 2 * P, :].rearrange("(p t) k -> p (t k)", p=P),
             )
 
         bo_cols = slice(N_QKV * D, (N_QKV + 1) * D)
@@ -165,11 +165,11 @@ def tile_block_pa_kernel(
 
         def copy_weight(copy, c, half):
             grouped_words = grouped_w[c][:].bitcast(F32).rearrange(
-                "q (t p u) -> q t p u", t=4, u=2
+                "q (h p t u) -> q h p t u", h=2, t=2, u=2
             )
             copy(
-                out=grouped_words[:, 2 * half : 2 * half + 2],
-                in_=w_bank[c, half][:].rearrange("q t u p -> q t p u"),
+                out=grouped_words[:, half],
+                in_=w_bank[c, half][:].rearrange("q t u p -> q p t u"),
             )
 
         def quantise_weight(c, codes, scales):
@@ -202,7 +202,6 @@ def tile_block_pa_kernel(
             )
 
         xb = {}
-        xb3 = []
         x_loc = [per_batch.tile([P, J, D], F32, name="x_loc") for b in range(B)]
         sums = [per_batch.tile([P, J], F32, name="sums") for b in range(B)]
         acc1 = {}
@@ -411,9 +410,9 @@ def tile_block_pa_kernel(
                 scale=ln_cols[:, t : t + 1],
             )
 
-        def regroup_h(b):
+        def regroup_h(copy, b):
             grouped_h[b] = per_batch.tile([P, J * P, PACK], BF16, align_bytes=64, name="grouped_h")
-            nc.vector.tensor_copy(
+            copy(
                 out=grouped_h[b][:].rearrange("q (c r) t -> q c t r", r=4),
                 in_=h_t[b][:].rearrange("q t (c r) -> q c t r", r=4),
             )
@@ -559,26 +558,26 @@ def tile_block_pa_kernel(
         turn_o(1)
         add_residual(0, 0)
         add_residual(0, 1)
-        mean(0, 0, 1)
-        mean(0, 1, 1)
-        deviations(0, 0)
-        deviations(0, 1)
-        inverse_deviation(0, 0, 1)
-        copy_o(1)
-        inverse_deviation(0, 1, 1)
-        copy_weight(on_vector, 0, 0)
-        copy_weight(on_vector, 0, 1)
-        normalise_on_vector(0, 0)
-        quantise_o(1)
-        normalise_on_vector(0, 1)
-        quantise_qkv_weight(0)
-        add_bias_to_x(nc.vector, 1, 0)
-        keep_busy(4)
         ln_bank = new_bank([P, P], "ln_bank")
         nc.tensor.transpose(ln_bank[:], ln_rows[:].bitcast(F32), ident[:])
-        turn_h_tile(0, 0)
+        mean(0, 0, 1)
+        deviations(0, 0)
+        mean(0, 1, 1)
+        inverse_deviation(0, 0, 1)
+        deviations(0, 1)
+        copy_o(1)
+        inverse_deviation(0, 1, 1)
         nc.scalar.copy(out=ln_pairs[:].bitcast(F32), in_=ln_bank[:, 0:PACK])
+        copy_weight(on_vector, 0, 0)
+        normalise_on_vector(0, 0)
+        copy_weight(on_vector, 0, 1)
+        quantise_o(1)
+        normalise_on_vector(0, 1)
         nc.scalar.copy(out=ln_cols[:], in_=ln_pairs[:])
+        quantise_qkv_weight(0)
+        add_bias_to_x(nc.vector, 1, 0)
+        keep_busy(3)
+        turn_h_tile(0, 0)
         gain_tile(0, 0)
         first_product(1)
         turn_h_tile(0, 1)
@@ -629,68 +628,70 @@ def tile_block_pa_kernel(
             gain_and_bias(1, t)
         add_residual(2, 0)
         add_residual(2, 1)
-        mean(2)
         turn_o(3)
         for j in range(J):
             sum_bias_and_x(3, j)
         copy_o(3)
+        mean(2)
+        copy_bias_and_x(3, 0)
+        copy_bias_and_x(3, 1)
         deviations(2, 0)
         deviations(2, 1)
         inverse_deviation(2)
-        copy_bias_and_x(3, 0)
-        copy_bias_and_x(3, 1)
         add_bias(0, 0, 2)
         add_bias(0, 1, 2)
-        regroup_h(1)
         quantise_o(3)
-        quantise_h(1)
+        regroup_h(on_vector, 1)
         first_product(3)
+        add_residual(3, 0)
+        quantise_h(1)
+        add_residual(3, 1)
+        keep_busy(2)
         second_product(1, 0)
+        add_bias(1, 0, 0)
         normalise_on_vector(2, 0)
         normalise_on_vector(2, 1)
-        add_bias(1, 0, 0)
-        turn_h(2)
-        second_product(1, 1)
-        add_residual(3, 0)
-        add_bias(1, 1, 0)
-        add_residual(3, 1)
         mean(3)
+        deviations(3, 0)
+        deviations(3, 1)
+        second_product(1, 1)
+        turn_h(2)
+        add_bias(1, 1, 0)
+        add_bias(1, 0, 1)
         for t in range(PACK):
             gain_and_bias(2, t)
-        second_product(1, 2)
-        deviations(3, 0)
-        add_bias(1, 1, 1)
-        deviations(3, 1)
         inverse_deviation(3)
-        add_bias(1, 0, 1)
-        regroup_h(2)
+        shifts(3)
+        normalise(3, 0)
+        normalise(3, 1)
+        second_product(1, 2)
+        add_bias(1, 1, 1)
+        regroup_h(on_vector, 2)
         add_bias(1, 0, 2)
         quantise_h(2)
         keep_busy(4)
+        turn_h(3)
         second_product(2, 0)
         add_bias(1, 1, 2)
-        normalise_on_vector(3, 0)
-        normalise_on_vector(3, 1)
-        turn_h(3)
-        second_product(2, 1)
-        add_bias(2, 0, 0)
         for t in range(PACK):
             gain_and_bias(3, t)
+        regroup_h(on_scalar, 3)
+        second_product(2, 1)
+        add_bias(2, 0, 0)
         add_bias(2, 1, 0)
         second_product(2, 2)
-        add_bias(2, 1, 1)
         add_bias(2, 0, 1)
-        regroup_h(3)
-        add_bias(2, 0, 2)
+        add_bias(2, 1, 1)
         quantise_h(3)
-        keep_busy(7)
+        add_bias(2, 0, 2)
+        add_bias(2, 1, 2)
+        keep_busy(2)
         second_product(3, 0)
         second_product(3, 1)
         second_product(3, 2)
-        add_bias(2, 1, 2)
         add_bias(3, 0, 0)
         add_bias(3, 1, 0)
-        add_bias(3, 0, 1)
+        add_bias_late(3, 0, 1)
         add_bias(3, 1, 1)
         for first in (0, 2):
             for j in range(J):

@@ -98,8 +98,8 @@ def tile_block_pa_kernel(
         load_row(bias_rows, 0, bo_cols, bo_l)
         for half in range(2):
             load_weight_half(wo_sb, Wo_l, half)
-        load_x(0)
         load_weight(wqkv_sb[0], Wqkv_g[0:D, :])
+        load_x(0)
         load_o(1)
         load_x(1)
         load_row(ln_rows, 0, slice(0, 2 * P), ln2_w, 2)
@@ -145,9 +145,11 @@ def tile_block_pa_kernel(
         w_bank = {}
         grouped_w = {}
 
-        def turn_weight(c, w_sb):
+        def turn_weight(c, w_sb, parts=range(2)):
             words = w_sb[:].bitcast(F32)
-            if c == 2:
+            if c in grouped_w:
+                pass
+            elif c == 2:
                 grouped_w[c] = shared.tile(
                     [P, PACK * D], BF16, align_bytes=64, name="grouped_w2", tag="late"
                 )
@@ -155,7 +157,7 @@ def tile_block_pa_kernel(
                 grouped_w[c] = per_weight.tile(
                     [P, PACK * D], BF16, align_bytes=64, name="grouped_w"
                 )
-            for half in range(2):
+            for half in parts:
                 w_bank[c, half] = new_bank([P, 2, 2, P], "w_bank")
                 for tt in range(2):
                     for u in range(2):
@@ -207,9 +209,14 @@ def tile_block_pa_kernel(
         acc1 = {}
 
         def add_bias_to_x(engine, b, j):
-            xb[b, j] = per_tile.tile([P, D], F32, name="xb")
+            if b == 2 and j == 0:
+                xb[b, j] = shared.tile([P, D], F32, name="xb2", tag="early", align_bytes=64)
+            elif b == 3 and j == 0:
+                xb[b, j] = shared.tile([P, 2 * D], F32, name="xb3", tag="late", align_bytes=64)
+            else:
+                xb[b, j] = per_tile.tile([P, D], F32, name="xb")
             engine.tensor_tensor(
-                out=xb[b, j][:],
+                out=xb[b, j][:, 0:D],
                 in0=x_sb[b][:, j * D : (j + 1) * D],
                 in1=bias_bc[:, bo_cols],
                 op=ALU.add,
@@ -252,7 +259,7 @@ def tile_block_pa_kernel(
                 out=x_loc[b][:, j, :],
                 in0=acc1[b, j][:],
                 scalar=1.0,
-                in1=xb[b, j][:],
+                in1=xb[b, j][:, 0:D],
                 op0=ALU.mult,
                 op1=ALU.add,
                 accum_out=sums[b][:, j : j + 1],
@@ -541,73 +548,74 @@ def tile_block_pa_kernel(
                 out=bias_bc[:, first * D : (first + width) * D], in_=bias_bank[first][:]
             )
 
+        keep_busy_plain(4)
         turn_o(0)
         copy_o(0)
         spread_bias(N_QKV, 1)
         copy_bias(on_vector, N_QKV, 1)
         quantise_o(0)
         turn_weight("o", wo_sb)
+        keep_busy_plain(2)
         copy_weight(on_scalar, "o", 0)
         copy_weight(on_scalar, "o", 1)
-        add_bias_to_x(nc.vector, 0, 0)
         quantise_wo_half(0)
         quantise_wo_half(1)
-        add_bias_to_x(nc.vector, 0, 1)
-        first_product(0)
+        for j in range(J):
+            add_bias_to_x(nc.vector, 0, j)
         turn_weight(0, wqkv_sb[0])
+        copy_weight(on_scalar, 0, 0)
+        copy_weight(on_scalar, 0, 1)
+        first_product(0)
         turn_o(1)
         add_residual(0, 0)
-        add_residual(0, 1)
         ln_bank = new_bank([P, P], "ln_bank")
         nc.tensor.transpose(ln_bank[:], ln_rows[:].bitcast(F32), ident[:])
         mean(0, 0, 1)
         deviations(0, 0)
+        add_residual(0, 1)
         mean(0, 1, 1)
         inverse_deviation(0, 0, 1)
+        nc.scalar.copy(out=ln_pairs[:].bitcast(F32), in_=ln_bank[:, 0:PACK])
         deviations(0, 1)
+        nc.scalar.copy(out=ln_cols[:], in_=ln_pairs[:])
         copy_o(1)
         inverse_deviation(0, 1, 1)
-        nc.scalar.copy(out=ln_pairs[:].bitcast(F32), in_=ln_bank[:, 0:PACK])
-        copy_weight(on_vector, 0, 0)
-        normalise_on_vector(0, 0)
-        copy_weight(on_vector, 0, 1)
-        quantise_o(1)
-        normalise_on_vector(0, 1)
-        nc.scalar.copy(out=ln_cols[:], in_=ln_pairs[:])
         quantise_qkv_weight(0)
+        normalise_on_vector(0, 0)
         add_bias_to_x(nc.vector, 1, 0)
-        keep_busy(3)
+        normalise_on_vector(0, 1)
+        quantise_o(1)
+        keep_busy(2)
         turn_h_tile(0, 0)
         gain_tile(0, 0)
-        first_product(1)
         turn_h_tile(0, 1)
         gain_tile(0, 1)
+        first_product(1)
         turn_weight(1, wqkv_sb[1])
         copy_weight(on_scalar, 1, 0)
         copy_weight(on_scalar, 1, 1)
         spread_bias(0, 2)
         copy_bias(on_scalar, 0, 2)
         turn_o(2)
-        add_residual(1, 0)
         regroup_tile(0, 0)
-        add_bias_to_x(nc.vector, 1, 1)
+        add_residual(1, 0)
         quantise_tile(0, 0)
+        add_bias_to_x(nc.vector, 1, 1)
+        regroup_tile(0, 1)
         add_residual(1, 1)
         mean(1)
-        regroup_tile(0, 1)
         quantise_qkv_weight(1)
         quantise_tile(0, 1)
         for j in range(J):
-            sum_bias_and_x(2, j)
+            add_bias_to_x(nc.gpsimd, 2, j)
         second_product(0, 0, [0])
+        keep_busy(2)
         second_product(0, 0, [1])
         second_product(0, 1)
+        copy_o(2)
         deviations(1, 0)
         deviations(1, 1)
-        copy_o(2)
         inverse_deviation(1)
-        copy_bias_and_x(2, 0)
-        copy_bias_and_x(2, 1)
         turn_weight(2, wqkv_sb[2])
         spread_bias(2, 1)
         keep_busy(2)
@@ -621,6 +629,8 @@ def tile_block_pa_kernel(
         normalise_on_vector(1, 0)
         normalise_on_vector(1, 1)
         quantise_qkv_weight(2)
+        for j in range(J):
+            add_bias_to_x(nc.gpsimd, 3, j)
         first_product(2)
         turn_h(1)
         second_product(0, 2)
@@ -629,12 +639,8 @@ def tile_block_pa_kernel(
         add_residual(2, 0)
         add_residual(2, 1)
         turn_o(3)
-        for j in range(J):
-            sum_bias_and_x(3, j)
         copy_o(3)
         mean(2)
-        copy_bias_and_x(3, 0)
-        copy_bias_and_x(3, 1)
         deviations(2, 0)
         deviations(2, 1)
         inverse_deviation(2)
@@ -642,6 +648,7 @@ def tile_block_pa_kernel(
         add_bias(0, 1, 2)
         quantise_o(3)
         regroup_h(on_vector, 1)
+        keep_busy(3)
         first_product(3)
         add_residual(3, 0)
         quantise_h(1)

@@ -76,10 +76,7 @@ def tile_block_pa_kernel(
             nc.sync.dma_start(out=x_sb[b][:], in_=x[b].rearrange("(p j) d -> p (j d)", j=J))
 
         def load_weight(w_sb, rows):
-            nc.sync.dma_start(
-                out=w_sb[:].rearrange("p (h f) -> p h f", h=2),
-                in_=rows.rearrange("(h p t) k -> p h (t k)", h=2, p=P),
-            )
+            nc.sync.dma_start(out=w_sb[:], in_=rows.rearrange("(p t) k -> p (t k)", p=P))
 
         def load_weight_half(w_sb, rows, half):
             nc.sync.dma_start(
@@ -166,9 +163,8 @@ def tile_block_pa_kernel(
                         )
 
         def copy_weight(copy, c, half):
-            grouped_words = grouped_w[c][:].bitcast(F32).rearrange(
-                "q (h p t u) -> q h p t u", h=2, t=2, u=2
-            )
+            pattern = "q (h p t u) -> q h p t u" if c == "o" else "q (p h t u) -> q h p t u"
+            grouped_words = grouped_w[c][:].bitcast(F32).rearrange(pattern, h=2, t=2, u=2)
             copy(
                 out=grouped_words[:, half],
                 in_=w_bank[c, half][:].rearrange("q t u p -> q p t u"),
@@ -468,11 +464,11 @@ def tile_block_pa_kernel(
 
         def store_when_complete(b, c):
             done.append((b, c))
-            if done.count((b, c)) == J:
-                store_heads(b, c)
+            if done.count((b, c)) == J and c != 1:
+                store_heads(nc.sync, b, c)
 
-        def store_heads(b, c):
-            nc.sync.dma_start(
+        def store_heads(queue, b, c):
+            queue.dma_start(
                 out=qkv_out[c][b].rearrange("n (p j) d -> p n (j d)", j=J),
                 in_=heads[b, c][:].rearrange("p n j d -> p n (j d)"),
             )
@@ -634,6 +630,7 @@ def tile_block_pa_kernel(
         first_product(2)
         turn_h(1)
         second_product(0, 2)
+        store_heads(nc.scalar, 0, 1)
         for t in range(PACK):
             gain_and_bias(1, t)
         add_residual(2, 0)
@@ -644,6 +641,8 @@ def tile_block_pa_kernel(
         deviations(2, 0)
         deviations(2, 1)
         inverse_deviation(2)
+        shift_tile(2, 0)
+        normalise(2, 0)
         add_bias(0, 0, 2)
         add_bias(0, 1, 2)
         quantise_o(3)
@@ -656,7 +655,6 @@ def tile_block_pa_kernel(
         keep_busy(2)
         second_product(1, 0)
         add_bias(1, 0, 0)
-        normalise_on_vector(2, 0)
         normalise_on_vector(2, 1)
         mean(3)
         deviations(3, 0)
@@ -667,12 +665,13 @@ def tile_block_pa_kernel(
         add_bias(1, 0, 1)
         for t in range(PACK):
             gain_and_bias(2, t)
+        add_bias(1, 1, 1)
         inverse_deviation(3)
+        store_heads(nc.scalar, 1, 1)
         shifts(3)
         normalise(3, 0)
         normalise(3, 1)
         second_product(1, 2)
-        add_bias(1, 1, 1)
         regroup_h(on_vector, 2)
         add_bias(1, 0, 2)
         quantise_h(2)
@@ -689,6 +688,7 @@ def tile_block_pa_kernel(
         second_product(2, 2)
         add_bias(2, 0, 1)
         add_bias(2, 1, 1)
+        store_heads(nc.scalar, 2, 1)
         quantise_h(3)
         add_bias(2, 0, 2)
         add_bias(2, 1, 2)
@@ -700,6 +700,7 @@ def tile_block_pa_kernel(
         add_bias(3, 1, 0)
         add_bias_late(3, 0, 1)
         add_bias(3, 1, 1)
+        store_heads(nc.scalar, 3, 1)
         for first in (0, 2):
             for j in range(J):
                 add_bias_heads(3, j, 2, first, 2)

@@ -574,16 +574,17 @@ def tile_block_pa_kernel(
         nc.scalar.copy(out=ln_pairs[:].bitcast(F32), in_=ln_bank[:, 0:PACK])
         deviations(0, 1)
         nc.scalar.copy(out=ln_cols[:], in_=ln_pairs[:])
-        copy_o(1)
         inverse_deviation(0, 1, 1)
+        copy_o(1)
         quantise_qkv_weight(0)
         normalise_on_vector(0, 0)
         add_bias_to_x(nc.vector, 1, 0)
         normalise_on_vector(0, 1)
         quantise_o(1)
-        keep_busy(2)
+        keep_busy(4)
         turn_h_tile(0, 0)
         gain_tile(0, 0)
+        keep_busy(1)
         turn_h_tile(0, 1)
         gain_tile(0, 1)
         first_product(1)
@@ -675,7 +676,7 @@ def tile_block_pa_kernel(
         regroup_h(on_vector, 2)
         add_bias(1, 0, 2)
         quantise_h(2)
-        keep_busy(4)
+        keep_busy(6)
         turn_h(3)
         second_product(2, 0)
         add_bias(1, 1, 2)

from contextlib import ExitStack

import concourse.mybir as mybir
from concourse.masks import make_identity

F32 = mybir.dt.float32
BF16 = mybir.dt.bfloat16
I32 = mybir.dt.int32
U32 = mybir.dt.uint32
U8 = mybir.dt.uint8
FP8X4 = mybir.dt.float8_e4m3fn_x4
ACT = mybir.ActivationFunctionType
ALU = mybir.AluOpType
RSQRT = ACT.Abs_reciprocal_sqrt

P = 128
B = 4
S = 256
D = 512
NH = 4
HD = 128
J = S // P
PACK = 4
WORDS = D // 2
N_QKV = 3
PSUM_BANKS = 8
EPS = 1e-5

FLOPS = 2 * B * S * D * (D + N_QKV * D)


def tile_block_pa_kernel(
    tc, o_loc, x, Wo_l, bo_l, ln2_w, ln2_b, Wqkv_g, bqkv_g, out_0, out_1, out_2, out_3
):
    nc = tc.nc
    qkv_out = [out_1, out_2, out_3]

    with ExitStack() as stack:
        keep = stack.enter_context(tc.tile_pool(name="keep", bufs=1))
        per_weight = stack.enter_context(tc.tile_pool(name="per_weight", bufs=1 + N_QKV))
        per_batch = stack.enter_context(tc.tile_pool(name="per_batch", bufs=B))
        per_tile = stack.enter_context(tc.tile_pool(name="per_tile", bufs=B * J))
        shared = stack.enter_context(tc.tile_pool(name="shared", bufs=1))
        results = stack.enter_context(tc.tile_pool(name="results", bufs=2 * N_QKV))
        banks = stack.enter_context(tc.psum_pool(name="banks", bufs=PSUM_BANKS - 1))
        spare = stack.enter_context(tc.psum_pool(name="spare", bufs=1))
        stack.enter_context(tc.manual_schedule())

        bias_rows = keep.tile([P, (N_QKV + 1) * D], BF16)
        nc.vector.memset(bias_rows[:, N_QKV * D :].bitcast(I32), 0)
        ln_rows = keep.tile([P, 2 * P], BF16)
        nc.vector.memset(ln_rows[:].bitcast(I32), 0)
        nc.vector.memset(bias_rows[:, 0 : N_QKV * D].bitcast(I32), 0)
        eps_col = keep.tile([P, 1], F32)
        nc.vector.memset(eps_col[:], EPS)
        ones = keep.tile([P, P], BF16)
        nc.vector.memset(ones[:], 1.0)
        zeros = keep.tile([P, D], BF16)
        nc.gpsimd.memset(zeros[:].bitcast(I32), 0)
        ident = keep.tile([P, P], F32)
        ident_bf = keep.tile([P, P], BF16)

        o_sb = [keep.tile([P, J * D], BF16, name="o_sb%d" % b) for b in range(B)]
        x_sb = [keep.tile([P, J * D], BF16, name="x_sb%d" % b) for b in range(B)]
        wo_sb = keep.tile([P, 4 * D], BF16)
        wqkv_sb = [keep.tile([P, 4 * D], BF16, name="wqkv_sb%d" % c) for c in range(N_QKV)]

        def load_o(b):
            for j in range(J):
                nc.sync.dma_start(
                    out=o_sb[b][:, j * D : (j + 1) * D].rearrange("p (n d) -> p n d", n=NH),
                    in_=o_loc[b].rearrange("n (p j) d -> p j n d", j=J)[:, j],
                )

        def load_x(b):
            nc.sync.dma_start(out=x_sb[b][:], in_=x[b].rearrange("(p j) d -> p (j d)", j=J))

        def load_weight(w_sb, rows):
            nc.sync.dma_start(out=w_sb[:], in_=rows.rearrange("(p t) k -> p (t k)", p=P))

        def load_weight_half(w_sb, rows, half):
            nc.sync.dma_start(
                out=w_sb[:, half * 2 * D : (half + 1) * 2 * D],
                in_=rows[half * 2 * P : (half + 1) * 2 * P, :].rearrange("(p t) k -> p (t k)", p=P),
            )

        bo_cols = slice(N_QKV * D, (N_QKV + 1) * D)
        make_identity(nc, ident[:])
        def load_row(tile, row, cols, vector, rows=1):
            nc.sync.dma_start(
                out=tile[row : row + rows, cols], in_=vector.rearrange("(u c) -> u c", u=rows)
            )

        load_o(0)
        load_row(bias_rows, 0, bo_cols, bo_l)
        for half in range(2):
            load_weight_half(wo_sb, Wo_l, half)
        load_weight(wqkv_sb[0], Wqkv_g[0:D, :])
        load_x(0)
        load_o(1)
        load_x(1)
        load_row(ln_rows, 0, slice(0, 2 * P), ln2_w, 2)
        load_row(ln_rows, 2, slice(0, 2 * P), ln2_b, 2)
        load_weight(wqkv_sb[1], Wqkv_g[D : 2 * D, :])
        load_row(bias_rows, 0, slice(0, N_QKV * D), bqkv_g)
        load_weight(wqkv_sb[2], Wqkv_g[2 * D : 3 * D, :])
        for b in range(2, B):
            load_o(b)
            load_x(b)

        nc.vector.tensor_copy(out=ident_bf[:], in_=ident[:])

        warm = keep.tile([P, 1], F32)
        nc.scalar.activation(out=warm[:], in_=eps_col[:], func=RSQRT)

        def new_bank(shape, name, dtype=F32):
            return banks.tile(shape, dtype, name=name, tag="bank")

        def turn_words(bank, words, first_word):
            nc.tensor.transpose(bank, words[:, first_word : first_word + P], ident[:])

        spare_bank = spare.tile([P, D], F32)

        def keep_busy_plain(count):
            for i in range(count):
                nc.tensor.matmul(
                    out=spare_bank[:], lhsT=ones[:], rhs=zeros[:], start=True, stop=True
                )

        def keep_busy(count):
            for i in range(count):
                nc.tensor.matmul_mx(
                    out=spare_bank[:],
                    lhsT=o_codes[0][:, 0:P].bitcast(FP8X4),
                    lhsT_scale=o_scales[0][:, 0:P],
                    rhs=wo_codes[:].bitcast(FP8X4),
                    rhs_scale=wo_scales[:],
                    start=True,
                    stop=True,
                )

        w_bank = {}
        grouped_w = {}

        def turn_weight(c, w_sb, parts=range(2)):
            words = w_sb[:].bitcast(F32)
            if c in grouped_w:
                pass
            elif c == 2:
                grouped_w[c] = shared.tile(
                    [P, PACK * D], BF16, align_bytes=64, name="grouped_w2", tag="late"
                )
            else:
                grouped_w[c] = per_weight.tile(
                    [P, PACK * D], BF16, align_bytes=64, name="grouped_w"
                )
            for half in parts:
                w_bank[c, half] = new_bank([P, 2, 2, P], "w_bank")
                for tt in range(2):
                    for u in range(2):
                        turn_words(
                            w_bank[c, half][:, tt, u, :], words, (2 * half + tt) * WORDS + u * P
                        )

        def copy_weight(copy, c, half):
            pattern = "q (h p t u) -> q h p t u" if c == "o" else "q (p h t u) -> q h p t u"
            grouped_words = grouped_w[c][:].bitcast(F32).rearrange(pattern, h=2, t=2, u=2)
            copy(
                out=grouped_words[:, half],
                in_=w_bank[c, half][:].rearrange("q t u p -> q p t u"),
            )

        def quantise_weight(c, codes, scales):
            nc.vector.quantize_mx(out=codes.bitcast(FP8X4), scales=scales, in_=grouped_w[c][:])

        o_bank = [None] * B
        grouped_o = [None] * B
        o_codes = [None] * B
        o_scales = [None] * B

        def turn_o(b):
            words = o_sb[b][:].bitcast(F32)
            o_bank[b] = new_bank([P, J, 2, P], "o_bank")
            for j in range(J):
                for u in range(2):
                    turn_words(o_bank[b][:, j, u, :], words, j * WORDS + u * P)

        def copy_o(b):
            grouped_o[b] = per_batch.tile([P, J * D], BF16, align_bytes=64, name="grouped_o")
            nc.scalar.copy(
                out=grouped_o[b][:].bitcast(F32).rearrange("q (j s u) -> q j s u", j=J, u=2),
                in_=o_bank[b][:].rearrange("q j u s -> q j s u"),
            )

        def quantise_o(b):
            o_codes[b] = per_batch.tile([P, J * P], U32, align_bytes=64, name="o_codes")
            o_scales[b] = per_batch.tile([P, J * P], U8, align_bytes=64, name="o_scales")
            nc.vector.quantize_mx(
                out=o_codes[b][:].bitcast(FP8X4), scales=o_scales[b][:], in_=grouped_o[b][:]
            )

        xb = {}
        x_loc = [per_batch.tile([P, J, D], F32, name="x_loc") for b in range(B)]
        sums = [per_batch.tile([P, J], F32, name="sums") for b in range(B)]
        acc1 = {}

        def add_bias_to_x(engine, b, j):
            if b == 2 and j == 0:
                xb[b, j] = shared.tile([P, D], F32, name="xb2", tag="early", align_bytes=64)
            elif b == 3 and j == 0:
                xb[b, j] = shared.tile([P, 2 * D], F32, name="xb3", tag="late", align_bytes=64)
            else:
                xb[b, j] = per_tile.tile([P, D], F32, name="xb")
            engine.tensor_tensor(
                out=xb[b, j][:, 0:D],
                in0=x_sb[b][:, j * D : (j + 1) * D],
                in1=bias_bc[:, bo_cols],
                op=ALU.add,
            )

        x_bank = {}

        def sum_bias_and_x(b, j):
            x_bank[b, j] = new_bank([P, D], "x_bank")
            nc.tensor.matmul(
                out=x_bank[b, j][:],
                lhsT=ident_bf[:],
                rhs=x_sb[b][:, j * D : (j + 1) * D],
                start=True,
                stop=False,
            )
            nc.tensor.matmul(
                out=x_bank[b, j][:], lhsT=ones[:], rhs=bias_rows[:, bo_cols], start=False, stop=True
            )

        def copy_bias_and_x(b, j):
            xb[b, j] = per_tile.tile([P, D], F32, name="xb")
            nc.scalar.copy(out=xb[b, j][:], in_=x_bank[b, j][:])

        def first_product(b):
            for j in range(J):
                acc1[b, j] = new_bank([P, D], "acc1")
                nc.tensor.matmul_mx(
                    out=acc1[b, j][:],
                    lhsT=o_codes[b][:, j * P : (j + 1) * P].bitcast(FP8X4),
                    lhsT_scale=o_scales[b][:, j * P : (j + 1) * P],
                    rhs=wo_codes[:].bitcast(FP8X4),
                    rhs_scale=wo_scales[:],
                    start=True,
                    stop=True,
                )

        def add_residual(b, j):
            nc.vector.scalar_tensor_tensor(
                out=x_loc[b][:, j, :],
                in0=acc1[b, j][:],
                scalar=1.0,
                in1=xb[b, j][:, 0:D],
                op0=ALU.mult,
                op1=ALU.add,
                accum_out=sums[b][:, j : j + 1],
            )
            if j == J - 1:
                nc.sync.dma_start(
                    out=out_0[b].rearrange("(p j) d -> p (j d)", j=J),
                    in_=x_loc[b][:].rearrange("p j d -> p (j d)"),
                )

        neg_mean = [None] * B
        sum_sq = [None] * B
        rstd = [None] * B
        shift = [None] * B
        normed = {}
        h_bank = {}
        h_t = [None] * B
        grouped_h = [None] * B
        h_codes = [None] * B
        h_scales = [None] * B

        def new_statistics(b):
            neg_mean[b] = per_batch.tile([P, J], F32, name="neg_mean")
            sum_sq[b] = per_batch.tile([P, J], F32, name="sum_sq")
            shift[b] = per_batch.tile([P, J], F32, name="shift")

        def mean(b, first=0, count=J):
            if first == 0:
                new_statistics(b)
            nc.scalar.mul(
                out=neg_mean[b][:, first : first + count],
                in_=sums[b][:, first : first + count],
                mul=-1.0 / D,
            )

        def deviations(b, j):
            squares = per_tile.tile([P, D], BF16, name="squares")
            nc.scalar.activation(
                out=squares[:],
                in_=x_loc[b][:, j, :],
                func=ACT.Square,
                bias=neg_mean[b][:, j : j + 1],
                scale=1.0,
                accum_out=sum_sq[b][:, j : j + 1],
            )

        def inverse_deviation(b, first=0, count=J):
            if first == 0:
                rstd[b] = per_batch.tile([P, J], F32, name="rstd")
            nc.scalar.activation(
                out=rstd[b][:, first : first + count],
                in_=sum_sq[b][:, first : first + count],
                func=RSQRT,
                bias=eps_col[:],
                scale=1.0 / D,
            )

        def shift_tile(b, j):
            nc.scalar.activation(
                out=shift[b][:, j : j + 1],
                in_=neg_mean[b][:, j : j + 1],
                func=ACT.Copy,
                scale=rstd[b][:, j : j + 1],
            )

        def shifts(b):
            for j in range(J):
                shift_tile(b, j)

        def normalise(b, j):
            normed[b, j] = per_tile.tile([P, 2, WORDS], F32, name="normed")
            nc.scalar.activation(
                out=normed[b, j][:],
                in_=x_loc[b][:, j, :].rearrange("p (c e) -> p e c", e=2),
                func=ACT.Identity,
                bias=shift[b][:, j : j + 1],
                scale=rstd[b][:, j : j + 1],
            )

        def normalise_on_vector(b, j):
            normed[b, j] = per_tile.tile([P, 2, WORDS], F32, name="normed")
            nc.vector.tensor_scalar(
                out=normed[b, j][:],
                in0=x_loc[b][:, j, :].rearrange("p (c e) -> p e c", e=2),
                scalar1=neg_mean[b][:, j : j + 1],
                scalar2=rstd[b][:, j : j + 1],
                op0=ALU.add,
                op1=ALU.mult,
            )

        def turn_h(b):
            for u in range(2):
                h_bank[b, u] = new_bank([P, 2, J, P], "h_bank")
            for j in range(J):
                for u in range(2):
                    for e in range(2):
                        nc.tensor.transpose(
                            h_bank[b, u][:, e, j, :],
                            normed[b, j][:, e, u * P : (u + 1) * P],
                            ident[:],
                        )
            h_t[b] = per_batch.tile([P, PACK, J * P], BF16, name="h_t")

        def turn_h_tile(b, j):
            h_bank[b, j] = new_bank([P, PACK, P], "h_bank")
            for u in range(2):
                for e in range(2):
                    nc.tensor.transpose(
                        h_bank[b, j][:, 2 * u + e, :],
                        normed[b, j][:, e, u * P : (u + 1) * P],
                        ident[:],
                    )
            if j == 0:
                h_t[b] = per_batch.tile([P, PACK, J * P], BF16, name="h_t")

        def gain_tile(b, j):
            for t in range(PACK):
                nc.scalar.activation(
                    out=h_t[b][:, t, j * P : (j + 1) * P],
                    in_=h_bank[b, j][:, t, :],
                    func=ACT.Identity,
                    bias=ln_cols[:, PACK + t : PACK + t + 1],
                    scale=ln_cols[:, t : t + 1],
                )

        def regroup_tile(b, j):
            if j == 0:
                grouped_h[b] = shared.tile(
                    [P, J * P, PACK], BF16, align_bytes=64, name="grouped_h0", tag="early"
                )
            tokens = slice(j * P, (j + 1) * P)
            nc.vector.tensor_copy(
                out=grouped_h[b][:, tokens, :].rearrange("q (c r) t -> q c t r", r=4),
                in_=h_t[b][:, :, tokens].rearrange("q t (c r) -> q c t r", r=4),
            )

        def quantise_tile(b, j):
            if j == 0:
                h_codes[b] = per_batch.tile([P, J * P], U32, align_bytes=64, name="h_codes")
                h_scales[b] = per_batch.tile([P, J * P], U8, align_bytes=64, name="h_scales")
            tokens = slice(j * P, (j + 1) * P)
            nc.vector.quantize_mx(
                out=h_codes[b][:, tokens].bitcast(FP8X4),
                scales=h_scales[b][:, tokens],
                in_=grouped_h[b][:, tokens, :].rearrange("q s t -> q (s t)"),
            )

        def gain_and_bias(b, t):
            u, e = divmod(t, 2)
            nc.scalar.activation(
                out=h_t[b][:, t, :],
                in_=h_bank[b, u][:, e, :, :].rearrange("q j s -> q (j s)"),
                func=ACT.Identity,
                bias=ln_cols[:, PACK + t : PACK + t + 1],
                scale=ln_cols[:, t : t + 1],
            )

        def regroup_h(copy, b):
            grouped_h[b] = per_batch.tile([P, J * P, PACK], BF16, align_bytes=64, name="grouped_h")
            copy(
                out=grouped_h[b][:].rearrange("q (c r) t -> q c t r", r=4),
                in_=h_t[b][:].rearrange("q t (c r) -> q c t r", r=4),
            )

        def quantise_h(b):
            h_codes[b] = per_batch.tile([P, J * P], U32, align_bytes=64, name="h_codes")
            h_scales[b] = per_batch.tile([P, J * P], U8, align_bytes=64, name="h_scales")
            nc.vector.quantize_mx(
                out=h_codes[b][:].bitcast(FP8X4),
                scales=h_scales[b][:],
                in_=grouped_h[b][:].rearrange("q s t -> q (s t)"),
            )

        acc2 = {}
        heads = {}

        def second_product(b, c, tiles=range(J)):
            cols = slice(c * D, (c + 1) * D)
            for j in tiles:
                acc2[b, j, c] = new_bank([P, D], "acc2")
                nc.tensor.matmul_mx(
                    out=acc2[b, j, c][:],
                    lhsT=h_codes[b][:, j * P : (j + 1) * P].bitcast(FP8X4),
                    lhsT_scale=h_scales[b][:, j * P : (j + 1) * P],
                    rhs=wqkv_codes[:, cols].bitcast(FP8X4),
                    rhs_scale=wqkv_scales[:, cols],
                    start=True,
                    stop=True,
                )

        def add_bias_late(b, j, c):
            cols = slice(c * D, (c + 1) * D)
            if (b, c) not in heads:
                heads[b, c] = results.tile([P, NH, J, HD], F32, name="heads")
            product = per_tile.tile([P, D], F32, name="product")
            nc.scalar.copy(out=product[:], in_=acc2[b, j, c][:])
            nc.gpsimd.tensor_tensor(
                out=heads[b, c][:, :, j, :],
                in0=product[:].rearrange("p (n d) -> p n d", n=NH),
                in1=bias_bc[:, cols].rearrange("p (n d) -> p n d", n=NH),
                op=ALU.add,
            )
            store_when_complete(b, c)

        done = []

        def store_when_complete(b, c):
            done.append((b, c))
            if done.count((b, c)) == J and c != 1:
                store_heads(nc.sync, b, c)

        def store_heads(queue, b, c):
            queue.dma_start(
                out=qkv_out[c][b].rearrange("n (p j) d -> p n (j d)", j=J),
                in_=heads[b, c][:].rearrange("p n j d -> p n (j d)"),
            )

        def add_bias_heads(b, j, c, first, count):
            cols = slice(c * D + first * HD, c * D + (first + count) * HD)
            if (b, c) not in heads:
                heads[b, c] = results.tile([P, NH, J, HD], F32, name="heads")
            nc.vector.tensor_tensor(
                out=heads[b, c][:, first : first + count, j, :],
                in0=acc2[b, j, c][:, first * HD : (first + count) * HD].rearrange(
                    "p (n d) -> p n d", n=count
                ),
                in1=bias_bc[:, cols].rearrange("p (n d) -> p n d", n=count),
                op=ALU.add,
            )
            if j == J - 1:
                nc.sync.dma_start(
                    out=qkv_out[c][b, first : first + count].rearrange("n (p j) d -> p n (j d)", j=J),
                    in_=heads[b, c][:, first : first + count].rearrange("p n j d -> p n (j d)"),
                )

        def add_bias(b, j, c):
            cols = slice(c * D, (c + 1) * D)
            if (b, c) not in heads:
                heads[b, c] = results.tile([P, NH, J, HD], F32, name="heads")
            nc.vector.tensor_tensor(
                out=heads[b, c][:, :, j, :],
                in0=acc2[b, j, c][:].rearrange("p (n d) -> p n d", n=NH),
                in1=bias_bc[:, cols].rearrange("p (n d) -> p n d", n=NH),
                op=ALU.add,
            )
            store_when_complete(b, c)

        bias_bc = keep.tile([P, (N_QKV + 1) * D], BF16)
        wo_codes = keep.tile([P, D], U32, align_bytes=64)
        wo_scales = keep.tile([P, D], U8, align_bytes=64)
        wqkv_codes = keep.tile([P, N_QKV * D], U32, align_bytes=64)
        wqkv_scales = keep.tile([P, N_QKV * D], U8, align_bytes=64)
        ln_pairs = keep.tile([P, 2 * PACK], BF16)
        ln_cols = keep.tile([P, 2 * PACK], F32)
        on_scalar = nc.scalar.copy
        on_vector = nc.vector.tensor_copy

        def quantise_wo_half(half):
            cols = slice(half * 2 * P, (half + 1) * 2 * P)
            nc.vector.quantize_mx(
                out=wo_codes[:, cols].bitcast(FP8X4),
                scales=wo_scales[:, cols],
                in_=grouped_w["o"][:, half * 2 * D : (half + 1) * 2 * D],
            )

        def quantise_qkv_weight(c):
            cols = slice(c * D, (c + 1) * D)
            quantise_weight(c, wqkv_codes[:, cols], wqkv_scales[:, cols])

        bias_bank = {}

        def spread_bias(first, width):
            bias_bank[first] = new_bank([P, width * D], "bias_bank", BF16)
            for part in range(width):
                cols = slice((first + part) * D, (first + part + 1) * D)
                nc.tensor.matmul(
                    out=bias_bank[first][:, part * D : (part + 1) * D],
                    lhsT=ones[:],
                    rhs=bias_rows[:, cols],
                    start=True,
                    stop=True,
                )

        def copy_bias(copy, first, width):
            copy(
                out=bias_bc[:, first * D : (first + width) * D], in_=bias_bank[first][:]
            )

        keep_busy_plain(4)
        turn_o(0)
        copy_o(0)
        spread_bias(N_QKV, 1)
        copy_bias(on_vector, N_QKV, 1)
        quantise_o(0)
        turn_weight("o", wo_sb)
        keep_busy_plain(2)
        copy_weight(on_scalar, "o", 0)
        copy_weight(on_scalar, "o", 1)
        quantise_wo_half(0)
        quantise_wo_half(1)
        for j in range(J):
            add_bias_to_x(nc.vector, 0, j)
        turn_weight(0, wqkv_sb[0])
        copy_weight(on_scalar, 0, 0)
        copy_weight(on_scalar, 0, 1)
        first_product(0)
        turn_o(1)
        add_residual(0, 0)
        ln_bank = new_bank([P, P], "ln_bank")
        nc.tensor.transpose(ln_bank[:], ln_rows[:].bitcast(F32), ident[:])
        mean(0, 0, 1)
        deviations(0, 0)
        add_residual(0, 1)
        mean(0, 1, 1)
        inverse_deviation(0, 0, 1)
        nc.scalar.copy(out=ln_pairs[:].bitcast(F32), in_=ln_bank[:, 0:PACK])
        deviations(0, 1)
        nc.scalar.copy(out=ln_cols[:], in_=ln_pairs[:])
        inverse_deviation(0, 1, 1)
        copy_o(1)
        quantise_qkv_weight(0)
        normalise_on_vector(0, 0)
        add_bias_to_x(nc.vector, 1, 0)
        normalise_on_vector(0, 1)
        quantise_o(1)
        keep_busy(4)
        turn_h_tile(0, 0)
        gain_tile(0, 0)
        keep_busy(1)
        turn_h_tile(0, 1)
        gain_tile(0, 1)
        first_product(1)
        turn_weight(1, wqkv_sb[1])
        copy_weight(on_scalar, 1, 0)
        copy_weight(on_scalar, 1, 1)
        spread_bias(0, 2)
        copy_bias(on_scalar, 0, 2)
        turn_o(2)
        regroup_tile(0, 0)
        add_residual(1, 0)
        quantise_tile(0, 0)
        add_bias_to_x(nc.vector, 1, 1)
        regroup_tile(0, 1)
        add_residual(1, 1)
        mean(1)
        quantise_qkv_weight(1)
        quantise_tile(0, 1)
        for j in range(J):
            add_bias_to_x(nc.gpsimd, 2, j)
        second_product(0, 0, [0])
        keep_busy(2)
        second_product(0, 0, [1])
        second_product(0, 1)
        copy_o(2)
        deviations(1, 0)
        deviations(1, 1)
        inverse_deviation(1)
        turn_weight(2, wqkv_sb[2])
        spread_bias(2, 1)
        keep_busy(2)
        copy_weight(on_scalar, 2, 0)
        copy_weight(on_scalar, 2, 1)
        copy_bias(on_scalar, 2, 1)
        for c in range(2):
            for j in range(J):
                add_bias(0, j, c)
        quantise_o(2)
        normalise_on_vector(1, 0)
        normalise_on_vector(1, 1)
        quantise_qkv_weight(2)
        for j in range(J):
            add_bias_to_x(nc.gpsimd, 3, j)
        first_product(2)
        turn_h(1)
        second_product(0, 2)
        store_heads(nc.scalar, 0, 1)
        for t in range(PACK):
            gain_and_bias(1, t)
        add_residual(2, 0)
        add_residual(2, 1)
        turn_o(3)
        copy_o(3)
        mean(2)
        deviations(2, 0)
        deviations(2, 1)
        inverse_deviation(2)
        shift_tile(2, 0)
        normalise(2, 0)
        add_bias(0, 0, 2)
        add_bias(0, 1, 2)
        quantise_o(3)
        regroup_h(on_vector, 1)
        keep_busy(3)
        first_product(3)
        add_residual(3, 0)
        quantise_h(1)
        add_residual(3, 1)
        keep_busy(2)
        second_product(1, 0)
        add_bias(1, 0, 0)
        normalise_on_vector(2, 1)
        mean(3)
        deviations(3, 0)
        deviations(3, 1)
        second_product(1, 1)
        turn_h(2)
        add_bias(1, 1, 0)
        add_bias(1, 0, 1)
        for t in range(PACK):
            gain_and_bias(2, t)
        add_bias(1, 1, 1)
        inverse_deviation(3)
        store_heads(nc.scalar, 1, 1)
        shifts(3)
        normalise(3, 0)
        normalise(3, 1)
        second_product(1, 2)
        regroup_h(on_vector, 2)
        add_bias(1, 0, 2)
        quantise_h(2)
        keep_busy(6)
        turn_h(3)
        second_product(2, 0)
        add_bias(1, 1, 2)
        for t in range(PACK):
            gain_and_bias(3, t)
        regroup_h(on_scalar, 3)
        second_product(2, 1)
        add_bias(2, 0, 0)
        add_bias(2, 1, 0)
        second_product(2, 2)
        add_bias(2, 0, 1)
        add_bias(2, 1, 1)
        store_heads(nc.scalar, 2, 1)
        quantise_h(3)
        add_bias(2, 0, 2)
        add_bias(2, 1, 2)
        keep_busy(2)
        second_product(3, 0)
        second_product(3, 1)
        second_product(3, 2)
        add_bias(3, 0, 0)
        add_bias(3, 1, 0)
        add_bias_late(3, 0, 1)
        add_bias(3, 1, 1)
        store_heads(nc.scalar, 3, 1)
        for first in (0, 2):
            for j in range(J):
                add_bias_heads(3, j, 2, first, 2)
